import numpy as np
import ml_dtypes


def mxq(x, axis, fmt="e4m3"):
    dtype, down = {"e4m3": (ml_dtypes.float8_e4m3fn, 7), "e5m2": (ml_dtypes.float8_e5m2, 14)}[fmt]
    v = np.moveaxis(np.asarray(x, np.float32).astype(ml_dtypes.bfloat16).astype(np.float64), axis, -1)
    blocks = v.reshape(v.shape[:-1] + (-1, 32))
    amax = np.abs(blocks).max(-1, keepdims=True)
    byte = np.maximum(np.where(amax > 0, np.frexp(amax)[1] - 1 + 127, 0) - down, 1)
    scale = np.exp2(byte - 127.0)
    codes = (blocks / scale).astype(np.float32).astype(dtype).astype(np.float64)
    return np.moveaxis((codes * scale).reshape(v.shape), -1, axis)


WIDE = False


def mx_kscale(k):
    if not WIDE:
        return np.ones(k)
    levels = np.array([10, -10, 5, -5, 0])
    if k % 512:
        return np.exp2(np.random.permutation(np.resize(levels, k // 32))).repeat(32)
    a = np.empty((k // 512, 16))
    for p in range(k // 512):
        a[p, :8] = np.random.permutation(np.resize(levels, 8))
        for g in range(8):
            far = levels[np.abs(levels - a[p, g]) >= 10]
            a[p, g + 8] = far[np.random.randint(len(far))]
    return np.exp2(a.ravel()).repeat(32)


BF16 = ml_dtypes.bfloat16


def bf(x):
    return np.asarray(x, np.float32).astype(BF16)


def f64(x):
    return np.asarray(x).astype(np.float64)


NA, NB, ND, ED = 64, 64, 1024, 512
K1 = 2 * ED


def setup_inputs():
    s, t = mx_kscale(K1), mx_kscale(ED)
    return {"edge_embeds": bf(np.random.standard_normal((NA, NB, K1)) * s),
            "a_proj": bf(np.random.standard_normal((NA, ED)) * 0.5 * t),
            "b_proj": bf(np.random.standard_normal((NB, ED)) * 0.5 * t),
            "We": bf(np.random.standard_normal((K1, ED)) * 0.7 / np.sqrt(K1) / s[:, None] * t),
            "be1": bf(np.random.standard_normal(ED) * 0.3 * t),
            "We2": bf(np.random.standard_normal((ED, ED)) * 0.5 / np.sqrt(ED) / t[:, None]),
            "be2": bf(np.random.standard_normal(ED) * 0.1)}


def reference(edge_embeds, a_proj, b_proj, We, be1, We2, be2):
    h = f64(a_proj)[:, None, :] + f64(b_proj)[None, :, :] + (mxq(f64(edge_embeds), 2, "e4m3") @ mxq(f64(We), 0, "e4m3")) + f64(be1)
    h = np.maximum(h, 0.0)
    edge_latent = np.maximum((mxq(h, 2, "e4m3") @ mxq(f64(We2), 0, "e4m3")) + f64(be2), 0.0)
    sum_a = edge_latent.sum(axis=1)
    sum_b = edge_latent.sum(axis=0)
    return edge_latent, sum_a, sum_b

@@ -1,0 +1,359 @@
+from contextlib import ExitStack
+
+import concourse.mybir as mybir
+from concourse.masks import make_identity
+
+F32 = mybir.dt.float32
+BF16 = mybir.dt.bfloat16
+U32 = mybir.dt.uint32
+U8 = mybir.dt.uint8
+FP8X4 = mybir.dt.float8_e4m3fn_x4
+ADD = mybir.AluOpType.add
+AX_X = mybir.AxisListType.X
+RELU = mybir.ActivationFunctionType.Relu
+
+P = 128
+NA = 64
+NB = 64
+K1 = 1024
+ED = 512
+BLOCKS = ED // P
+PACK = 4
+PASSES = K1 // (P * PACK)
+BANK = 512
+PAIR = 2 * P
+FLOPS = 2 * NA * NB * K1 * ED + 2 * NA * NB * ED * ED
+
+TILES = (2, 2, 4, 4, 4, 4, 4, 4, 2, 2)
+VECTOR_SUM_BLOCKS = 3
+ACC_LAG = 3
+
+
+def tile_bipartiteneuralmessagepassinglayer_pa_t_kernel(
+    tc, edge_embeds, a_proj, b_proj, We, be1, We2, be2, out_0, out_1, out_2
+):
+    nc = tc.nc
+    x_rows = edge_embeds.rearrange("i j k -> (i j) k")
+    o_rows = out_0.rearrange("i j f -> (i j) f")
+    NC = len(TILES)
+    first_tile = [sum(TILES[:c]) for c in range(NC)]
+    assert sum(TILES) * P == NA * NB
+
+    with ExitStack() as ctx:
+        const = ctx.enter_context(tc.tile_pool(name="const", bufs=1))
+        work = ctx.enter_context(tc.tile_pool(name="work", bufs=2))
+        psum = ctx.enter_context(tc.psum_pool(name="psum", bufs=7))
+        psacc = ctx.enter_context(tc.psum_pool(name="psacc", bufs=1))
+        ctx.enter_context(tc.manual_schedule())
+
+        def bank(label):
+            return psum.tile([P, BANK], F32, tag="bank", name=label)
+
+        ab_bf = const.tile([P, ED], BF16, name="ab_bf")
+        bias_bf = const.tile([P, P], BF16, name="bias_bf")
+        be1_bf = const.tile([P, PACK], BF16, name="be1_bf")
+        nc.vector.memset(bias_bf[:], 0.0)
+        nc.scalar.dma_start(out=ab_bf[0:NA, :], in_=a_proj)
+        nc.scalar.dma_start(out=ab_bf[NA:P, :], in_=b_proj)
+        nc.scalar.dma_start(out=be1_bf[:], in_=be1.rearrange("(p t) -> p t", t=PACK))
+        nc.scalar.dma_start(out=bias_bf[0:BLOCKS, :], in_=be2.rearrange("(m f) -> m f", m=BLOCKS))
+        ident = const.tile([P, P], F32, name="ident")
+        make_identity(nc, ident[:])
+        acc = psacc.tile([P, ED], F32, name="acc")
+
+        xs = []
+        for c in range(NC):
+            xs.append(const.tile([P, TILES[c], K1], BF16, name="x%d" % c))
+        wraw = const.tile([P, PASSES, PACK, ED], BF16, name="wraw")
+        w2raw = const.tile([P, PACK, ED], BF16, name="w2raw")
+
+        def load_x(c):
+            r0 = first_tile[c] * P
+            rows = x_rows[r0 : r0 + TILES[c] * P, :]
+            nc.sync.dma_start(out=xs[c][:], in_=rows.rearrange("(t p) k -> p t k", p=P))
+
+        def load_w(g):
+            rows = We[g * P * PACK : (g + 1) * P * PACK, :]
+            nc.sync.dma_start(out=wraw[:, g, :, :], in_=rows.rearrange("(p t) c -> p t c", t=PACK))
+
+        load_w(0)
+        load_w(1)
+        load_x(0)
+        load_x(1)
+        nc.sync.dma_start(out=w2raw[:], in_=We2.rearrange("(p t) c -> p t c", t=PACK))
+        for c in range(2, NC):
+            load_x(c)
+
+        ab32 = const.tile([P, ED], F32, name="ab32")
+        bias32 = const.tile([P, P], F32, name="bias32")
+        be1T = const.tile([P, PACK], F32, name="be1T")
+        biasT = const.tile([P, BLOCKS], F32, name="biasT")
+        abT = const.tile([P, PACK, P], F32, name="abT")
+        st = const.tile([P, BLOCKS, P], F32, name="st")
+        sel = const.tile([P, P], F32, name="sel")
+
+        def small_inputs_cast():
+            nc.vector.tensor_copy(out=ab32[:], in_=ab_bf[:])
+            nc.vector.tensor_copy(out=bias32[:], in_=bias_bf[:])
+            nc.vector.tensor_copy(out=be1T[:], in_=be1_bf[:])
+
+        def small_inputs_transpose():
+            ps_ab = bank("ps_ab")
+            for t in range(PACK):
+                nc.tensor.transpose(ps_ab[:, t * P : (t + 1) * P], ab32[:, t:ED:PACK], ident[:])
+            ps_bias = bank("ps_bias")
+            nc.tensor.transpose(ps_bias[:, 0:P], bias32[:], ident[:])
+            return ps_ab, ps_bias
+
+        def small_inputs_finish(ps_ab, ps_bias):
+            nc.vector.tensor_copy(out=biasT[:], in_=ps_bias[:, 0:BLOCKS])
+            nc.vector.tensor_copy(
+                out=abT[:, :, 0:NA], in_=ps_ab[:].rearrange("p (m r) -> p m r", m=BLOCKS)[:, :, 0:NA]
+            )
+            for m in range(BLOCKS):
+                nc.vector.tensor_scalar_add(
+                    out=abT[:, m, NA:P], in0=ps_ab[:, m * P + NA : (m + 1) * P], scalar1=be1T[:, m : m + 1]
+                )
+            nc.vector.memset(st[:], 0.0)
+            nc.vector.tensor_tensor(out=sel[:, 0:NB], in0=ident[:, 0:NB], in1=ident[:, NB:P], op=ADD)
+            nc.vector.tensor_tensor(out=sel[:, NB:P], in0=ident[:, 0:NB], in1=ident[:, NB:P], op=ADD)
+
+        wg = const.tile([P, PASSES, ED, PACK], BF16, name="wg", align_bytes=64)
+        wq = const.tile([P, PASSES * ED], U32, name="wq", align_bytes=64)
+        wsc = const.tile([P, PASSES * ED], U8, name="wsc", align_bytes=64)
+        w2g = const.tile([P, ED, PACK], BF16, name="w2g", align_bytes=64)
+        w2q = const.tile([P, ED], U32, name="w2q", align_bytes=64)
+        w2sc = const.tile([P, ED], U8, name="w2sc", align_bytes=64)
+
+        def regroup(eng_copy, dst, src):
+            eng_copy(
+                out=dst.rearrange("p (c z) t -> p c t z", z=4),
+                in_=src.rearrange("p t (c z) -> p c t z", z=4),
+            )
+
+        def prep_we():
+            for g in range(PASSES):
+                nc.vector.tensor_copy(
+                    out=wg[:, g, :, :].rearrange("p (t m) j -> p t m j", t=PACK),
+                    in_=wraw[:, g, :, :].rearrange("p j (m t) -> p t m j", t=PACK),
+                )
+            nc.vector.quantize_mx(
+                out=wq[:].bitcast(FP8X4),
+                scales=wsc[:],
+                in_=wg[:].rearrange("p g c t -> p (g c t)"),
+            )
+
+        def prep_we2_regroup():
+            regroup(nc.scalar.copy, w2g[:], w2raw[:])
+
+        def prep_we2_quant():
+            nc.vector.quantize_mx(
+                out=w2q[:].bitcast(FP8X4), scales=w2sc[:], in_=w2g[:].rearrange("p c t -> p (c t)")
+            )
+
+        xg = {}
+        xq = {}
+        xsc = {}
+        yy = {}
+        hg = {}
+        hq = {}
+        hsc = {}
+        lt = {}
+        lo = {}
+
+        def live(c):
+            return 0 <= c < NC
+
+        def transpose_x(c):
+            n = TILES[c] * P
+            xg[c] = work.tile([P, PASSES, n, 2], F32, name="xg%d" % c, tag="xg", align_bytes=64)
+            for pair in range(TILES[c] // 2):
+                for g in range(PASSES):
+                    pb = bank("xt%d_%d_%d" % (c, g, pair))
+                    for u in range(2):
+                        for side in range(2):
+                            words = xs[c][:, 2 * pair + side, :].bitcast(F32)
+                            nc.tensor.transpose(
+                                pb[:, u * PAIR + side * P : u * PAIR + (side + 1) * P],
+                                words[:, 2 * P * g + u : 2 * P * (g + 1) : 2],
+                                ident[:],
+                            )
+                    nc.scalar.copy(
+                        out=xg[c][:, g, pair * PAIR : (pair + 1) * PAIR, :],
+                        in_=pb[:].rearrange("p (u e) -> p e u", u=2),
+                    )
+
+        def quant_x(c):
+            n = TILES[c] * P
+            xq[c] = work.tile([P, PASSES * n], U32, name="xq%d" % c, tag="xq", align_bytes=64)
+            xsc[c] = work.tile([P, PASSES * n], U8, name="xsc%d" % c, tag="xsc", align_bytes=64)
+            nc.vector.quantize_mx(
+                out=xq[c][:].bitcast(FP8X4),
+                scales=xsc[c][:],
+                in_=xg[c][:].rearrange("p g e u -> p (g e u)").bitcast(BF16),
+            )
+
+        def stage1(c, m):
+            n = TILES[c] * P
+            if m == 0:
+                yy[c] = work.tile([P, BLOCKS, n], BF16, name="y%d" % c, tag="y")
+            pb = bank("p1_%d_%d" % (c, m))
+            for g in range(PASSES):
+                cols = slice(g * ED + m * P, g * ED + (m + 1) * P)
+                nc.tensor.matmul_mx(
+                    out=pb[:, 0:n],
+                    lhsT=wq[:, cols].bitcast(FP8X4),
+                    lhsT_scale=wsc[:, cols],
+                    rhs=xq[c][:, g * n : (g + 1) * n].bitcast(FP8X4),
+                    rhs_scale=xsc[c][:, g * n : (g + 1) * n],
+                    start=(g == 0),
+                    stop=(g == PASSES - 1),
+                )
+            for il in range(2 * TILES[c]):
+                i = 2 * first_tile[c] + il
+                nc.vector.scalar_tensor_tensor(
+                    out=yy[c][:, m, il * NB : (il + 1) * NB],
+                    in0=pb[:, il * NB : (il + 1) * NB],
+                    scalar=abT[:, m, i : i + 1],
+                    in1=abT[:, m, NA:P],
+                    op0=ADD,
+                    op1=ADD,
+                )
+
+        def relu_regroup(c):
+            n = TILES[c] * P
+            hg[c] = work.tile([P, n, PACK], BF16, name="hg%d" % c, tag="hg", align_bytes=64)
+            nc.vector.tensor_scalar_max(
+                out=hg[c][:].rearrange("p (c z) t -> p c t z", z=4),
+                in0=yy[c][:].rearrange("p t (c z) -> p c t z", z=4),
+                scalar1=0.0,
+            )
+
+        def quant_h(c):
+            n = TILES[c] * P
+            hq[c] = work.tile([P, n], U32, name="hq%d" % c, tag="hq", align_bytes=64)
+            hsc[c] = work.tile([P, n], U8, name="hsc%d" % c, tag="hsc", align_bytes=64)
+            nc.vector.quantize_mx(
+                out=hq[c][:].bitcast(FP8X4),
+                scales=hsc[c][:],
+                in_=hg[c][:].rearrange("p e t -> p (e t)"),
+            )
+
+        def stage2(c, m):
+            n = TILES[c] * P
+            if m == 0:
+                lt[c] = work.tile([P, BLOCKS, n], F32, name="lt%d" % c, tag="lt", bufs=ACC_LAG)
+            pb = bank("p2_%d_%d" % (c, m))
+            cols = slice(m * P, (m + 1) * P)
+            nc.tensor.matmul_mx(
+                out=pb[:, 0:n],
+                lhsT=w2q[:, cols].bitcast(FP8X4),
+                lhsT_scale=w2sc[:, cols],
+                rhs=hq[c][:].bitcast(FP8X4),
+                rhs_scale=hsc[c][:],
+                start=True,
+                stop=True,
+            )
+            if m < VECTOR_SUM_BLOCKS:
+                nc.scalar.activation(
+                    out=lt[c][:, m, :], in_=pb[:, 0:n], func=RELU, bias=biasT[:, m : m + 1], scale=1.0
+                )
+            else:
+                for il in range(2 * TILES[c]):
+                    i = 2 * first_tile[c] + il
+                    nc.scalar.activation(
+                        out=lt[c][:, m, il * NB : (il + 1) * NB],
+                        in_=pb[:, il * NB : (il + 1) * NB],
+                        func=RELU,
+                        bias=biasT[:, m : m + 1],
+                        scale=1.0,
+                        accum_out=st[:, m, i : i + 1],
+                    )
+
+        def sum_a(c, m0, m1):
+            i0 = 2 * first_tile[c]
+            nc.vector.tensor_reduce(
+                out=st[:, m0:m1, i0 : i0 + 2 * TILES[c]],
+                in_=lt[c][:, m0:m1, :].rearrange("p m (i j) -> p m i j", j=NB),
+                axis=AX_X,
+                op=ADD,
+            )
+
+        def back(c):
+            lo[c] = work.tile([P, TILES[c], ED], F32, name="lo%d" % c, tag="lo")
+            r0 = first_tile[c] * P
+            for tl in range(TILES[c]):
+                pb = bank("lb%d_%d" % (c, tl))
+                for m in range(BLOCKS):
+                    nc.tensor.transpose(
+                        pb[:, m * P : (m + 1) * P], lt[c][:, m, tl * P : (tl + 1) * P], ident[:]
+                    )
+                nc.scalar.copy(out=lo[c][:, tl, :], in_=pb[:])
+                if c == NC - 1:
+                    nc.sync.dma_start(out=o_rows[r0 + tl * P : r0 + (tl + 1) * P, :], in_=lo[c][:, tl, :])
+            if c < NC - 1:
+                rows = o_rows[r0 : r0 + TILES[c] * P, :]
+                nc.sync.dma_start(out=rows.rearrange("(t p) f -> p t f", p=P), in_=lo[c][:])
+
+        def accumulate(c):
+            for tl in range(TILES[c]):
+                for m in range(BLOCKS):
+                    nc.tensor.matmul(
+                        out=acc[:, m * P : (m + 1) * P],
+                        lhsT=lt[c][:, m, tl * P : (tl + 1) * P],
+                        rhs=ident[:],
+                        is_transpose=True,
+                        start=(c == 0 and tl == 0 and m == 0),
+                        stop=(c == NC - 1 and tl == TILES[c] - 1 and m == BLOCKS - 1),
+                    )
+
+        prep_we()
+        transpose_x(0)
+        small_inputs_cast()
+        ps_small = small_inputs_transpose()
+        quant_x(0)
+        small_inputs_finish(ps_small[0], ps_small[1])
+        for k in range(NC + 2):
+            if live(k - 1):
+                relu_regroup(k - 1)
+            if live(k - ACC_LAG):
+                accumulate(k - ACC_LAG)
+            if k == NC + 1:
+                for c in range(k - ACC_LAG + 1, NC):
+                    accumulate(c)
+            if live(k + 1):
+                transpose_x(k + 1)
+            if live(k - 2):
+                sum_a(k - 2, 0, 2)
+            if live(k - 1):
+                quant_h(k - 1)
+            if live(k - 2):
+                back(k - 2)
+            if k == 0:
+                prep_we2_regroup()
+            if live(k):
+                for m in range(BLOCKS):
+                    stage1(k, m)
+            if live(k + 1):
+                quant_x(k + 1)
+            if k == 0:
+                prep_we2_quant()
+            if live(k - 1):
+                for m in range(BLOCKS):
+                    stage2(k - 1, m)
+            if live(k - 2):
+                sum_a(k - 2, 2, VECTOR_SUM_BLOCKS)
+
+        pa = bank("ps_suma")
+        for m in range(BLOCKS):
+            nc.tensor.transpose(pa[:, m * P : (m + 1) * P], st[:, m, :], ident[:])
+        so_a = const.tile([P, ED], F32, name="so_a")
+        nc.scalar.copy(out=so_a[:], in_=pa[:])
+        nc.sync.dma_start(out=out_1, in_=so_a[0:NA, :])
+        acc_sb = const.tile([P, ED], F32, name="acc_sb")
+        nc.vector.tensor_copy(out=acc_sb[:], in_=acc[:])
+        pb = bank("ps_sumb")
+        nc.tensor.matmul(out=pb[:], lhsT=sel[:], rhs=acc_sb[:], start=True, stop=True)
+        so_b = const.tile([P, ED], F32, name="so_b")
+        nc.vector.tensor_copy(out=so_b[:], in_=pb[:])
+        nc.sync.dma_start(out=out_2, in_=so_b[0:NB, :])

@@ -11,6 +11,7 @@ FP8X4 = mybir.dt.float8_e4m3fn_x4
 ADD = mybir.AluOpType.add
 AX_X = mybir.AxisListType.X
 RELU = mybir.ActivationFunctionType.Relu
+IDENTITY = mybir.ActivationFunctionType.Identity
 
 P = 128
 NA = 64
@@ -20,12 +21,14 @@ ED = 512
 BLOCKS = ED // P
 PACK = 4
 PASSES = K1 // (P * PACK)
+ALL_TILES = NA * NB // P
 BANK = 512
 PAIR = 2 * P
 FLOPS = 2 * NA * NB * K1 * ED + 2 * NA * NB * ED * ED
 
 TILES = (2, 2, 4, 4, 4, 4, 4, 4, 2, 2)
 VECTOR_SUM_BLOCKS = 3
+LAST = 2
 ACC_LAG = 3
 
 
@@ -37,7 +40,7 @@ def tile_bipartiteneuralmessagepassinglayer_pa_t_kernel(
     o_rows = out_0.rearrange("i j f -> (i j) f")
     NC = len(TILES)
     first_tile = [sum(TILES[:c]) for c in range(NC)]
-    assert sum(TILES) * P == NA * NB
+    assert sum(TILES) == ALL_TILES
 
     with ExitStack() as ctx:
         const = ctx.enter_context(tc.tile_pool(name="const", bufs=1))
@@ -61,28 +64,26 @@ def tile_bipartiteneuralmessagepassinglayer_pa_t_kernel(
         make_identity(nc, ident[:])
         acc = psacc.tile([P, ED], F32, name="acc")
 
-        xs = []
-        for c in range(NC):
-            xs.append(const.tile([P, TILES[c], K1], BF16, name="x%d" % c))
+        xs = const.tile([P, ALL_TILES, K1], BF16, name="xs")
         wraw = const.tile([P, PASSES, PACK, ED], BF16, name="wraw")
         w2raw = const.tile([P, PACK, ED], BF16, name="w2raw")
 
-        def load_x(c):
-            r0 = first_tile[c] * P
-            rows = x_rows[r0 : r0 + TILES[c] * P, :]
-            nc.sync.dma_start(out=xs[c][:], in_=rows.rearrange("(t p) k -> p t k", p=P))
+        def load_x(t):
+            rows = x_rows[t * P : (t + 2) * P, :]
+            nc.sync.dma_start(out=xs[:, t : t + 2, :], in_=rows.rearrange("(t p) k -> p t k", p=P))
 
         def load_w(g):
             rows = We[g * P * PACK : (g + 1) * P * PACK, :]
             nc.sync.dma_start(out=wraw[:, g, :, :], in_=rows.rearrange("(p t) c -> p t c", t=PACK))
 
+        load_x(0)
         load_w(0)
         load_w(1)
-        load_x(0)
-        load_x(1)
+        load_x(2)
+        load_x(4)
         nc.sync.dma_start(out=w2raw[:], in_=We2.rearrange("(p t) c -> p t c", t=PACK))
-        for c in range(2, NC):
-            load_x(c)
+        for t in range(6, ALL_TILES, 2):
+            load_x(t)
 
         ab32 = const.tile([P, ED], F32, name="ab32")
         bias32 = const.tile([P, P], F32, name="bias32")
@@ -91,11 +92,16 @@ def tile_bipartiteneuralmessagepassinglayer_pa_t_kernel(
         abT = const.tile([P, PACK, P], F32, name="abT")
         st = const.tile([P, BLOCKS, P], F32, name="st")
         sel = const.tile([P, P], F32, name="sel")
+        nc.gpsimd.memset(st[:], 0.0)
+        for half in range(2):
+            nc.gpsimd.tensor_tensor(
+                out=sel[:, half * NB : (half + 1) * NB], in0=ident[:, 0:NB], in1=ident[:, NB:P], op=ADD
+            )
 
         def small_inputs_cast():
-            nc.vector.tensor_copy(out=ab32[:], in_=ab_bf[:])
-            nc.vector.tensor_copy(out=bias32[:], in_=bias_bf[:])
-            nc.vector.tensor_copy(out=be1T[:], in_=be1_bf[:])
+            nc.scalar.copy(out=ab32[:], in_=ab_bf[:])
+            nc.scalar.copy(out=bias32[:], in_=bias_bf[:])
+            nc.scalar.copy(out=be1T[:], in_=be1_bf[:])
 
         def small_inputs_transpose():
             ps_ab = bank("ps_ab")
@@ -106,17 +112,18 @@ def tile_bipartiteneuralmessagepassinglayer_pa_t_kernel(
             return ps_ab, ps_bias
 
         def small_inputs_finish(ps_ab, ps_bias):
-            nc.vector.tensor_copy(out=biasT[:], in_=ps_bias[:, 0:BLOCKS])
-            nc.vector.tensor_copy(
-                out=abT[:, :, 0:NA], in_=ps_ab[:].rearrange("p (m r) -> p m r", m=BLOCKS)[:, :, 0:NA]
+            nc.scalar.copy(
+                out=abT[:, :, 0:NA], in_=ps_ab[:].rearrange("p (t r) -> p t r", t=PACK)[:, :, 0:NA]
             )
-            for m in range(BLOCKS):
-                nc.vector.tensor_scalar_add(
-                    out=abT[:, m, NA:P], in0=ps_ab[:, m * P + NA : (m + 1) * P], scalar1=be1T[:, m : m + 1]
+            for t in range(PACK):
+                nc.scalar.activation(
+                    out=abT[:, t, NA:P],
+                    in_=ps_ab[:, t * P + NA : (t + 1) * P],
+                    func=IDENTITY,
+                    bias=be1T[:, t : t + 1],
+                    scale=1.0,
                 )
-            nc.vector.memset(st[:], 0.0)
-            nc.vector.tensor_tensor(out=sel[:, 0:NB], in0=ident[:, 0:NB], in1=ident[:, NB:P], op=ADD)
-            nc.vector.tensor_tensor(out=sel[:, NB:P], in0=ident[:, 0:NB], in1=ident[:, NB:P], op=ADD)
+            nc.scalar.copy(out=biasT[:], in_=ps_bias[:, 0:BLOCKS])
 
         wg = const.tile([P, PASSES, ED, PACK], BF16, name="wg", align_bytes=64)
         wq = const.tile([P, PASSES * ED], U32, name="wq", align_bytes=64)
@@ -131,16 +138,18 @@ def tile_bipartiteneuralmessagepassinglayer_pa_t_kernel(
                 in_=src.rearrange("p t (c z) -> p c t z", z=4),
             )
 
-        def prep_we():
-            for g in range(PASSES):
-                nc.vector.tensor_copy(
-                    out=wg[:, g, :, :].rearrange("p (t m) j -> p t m j", t=PACK),
-                    in_=wraw[:, g, :, :].rearrange("p j (m t) -> p t m j", t=PACK),
-                )
+        def regroup_we(eng_copy, g, t0, t1):
+            eng_copy(
+                out=wg[:, g, t0 * P : t1 * P, :].rearrange("p (t m) j -> p t m j", m=P),
+                in_=wraw[:, g, :, :].rearrange("p j (m t) -> p t m j", t=PACK)[:, t0:t1, :, :],
+            )
+
+        def quant_we(g, t0, t1):
+            cols = slice(g * ED + t0 * P, g * ED + t1 * P)
             nc.vector.quantize_mx(
-                out=wq[:].bitcast(FP8X4),
-                scales=wsc[:],
-                in_=wg[:].rearrange("p g c t -> p (g c t)"),
+                out=wq[:, cols].bitcast(FP8X4),
+                scales=wsc[:, cols],
+                in_=wg[:, g, t0 * P : t1 * P, :].rearrange("p c t -> p (c t)"),
             )
 
         def prep_we2_regroup():
@@ -164,6 +173,9 @@ def tile_bipartiteneuralmessagepassinglayer_pa_t_kernel(
         def live(c):
             return 0 <= c < NC
 
+        def vector_sums(c):
+            return VECTOR_SUM_BLOCKS if c < NC - LAST else 0
+
         def transpose_x(c):
             n = TILES[c] * P
             xg[c] = work.tile([P, PASSES, n, 2], F32, name="xg%d" % c, tag="xg", align_bytes=64)
@@ -172,7 +184,7 @@ def tile_bipartiteneuralmessagepassinglayer_pa_t_kernel(
                     pb = bank("xt%d_%d_%d" % (c, g, pair))
                     for u in range(2):
                         for side in range(2):
-                            words = xs[c][:, 2 * pair + side, :].bitcast(F32)
+                            words = xs[:, first_tile[c] + 2 * pair + side, :].bitcast(F32)
                             nc.tensor.transpose(
                                 pb[:, u * PAIR + side * P : u * PAIR + (side + 1) * P],
                                 words[:, 2 * P * g + u : 2 * P * (g + 1) : 2],
@@ -254,7 +266,7 @@ def tile_bipartiteneuralmessagepassinglayer_pa_t_kernel(
                 start=True,
                 stop=True,
             )
-            if m < VECTOR_SUM_BLOCKS:
+            if m < vector_sums(c):
                 nc.scalar.activation(
                     out=lt[c][:, m, :], in_=pb[:, 0:n], func=RELU, bias=biasT[:, m : m + 1], scale=1.0
                 )
@@ -288,7 +300,8 @@ def tile_bipartiteneuralmessagepassinglayer_pa_t_kernel(
                     nc.tensor.transpose(
                         pb[:, m * P : (m + 1) * P], lt[c][:, m, tl * P : (tl + 1) * P], ident[:]
                     )
-                nc.scalar.copy(out=lo[c][:, tl, :], in_=pb[:])
+                back_copy = nc.scalar.copy if c < NC - LAST else nc.vector.tensor_copy
+                back_copy(out=lo[c][:, tl, :], in_=pb[:])
                 if c == NC - 1:
                     nc.sync.dma_start(out=o_rows[r0 + tl * P : r0 + (tl + 1) * P, :], in_=lo[c][:, tl, :])
             if c < NC - 1:
@@ -307,28 +320,36 @@ def tile_bipartiteneuralmessagepassinglayer_pa_t_kernel(
                         stop=(c == NC - 1 and tl == TILES[c] - 1 and m == BLOCKS - 1),
                     )
 
-        prep_we()
-        transpose_x(0)
+        half = PACK // 2
         small_inputs_cast()
+        transpose_x(0)
         ps_small = small_inputs_transpose()
-        quant_x(0)
         small_inputs_finish(ps_small[0], ps_small[1])
+        regroup_we(nc.vector.tensor_copy, 0, 0, PACK)
+        regroup_we(nc.vector.tensor_copy, 1, 0, half)
+        regroup_we(nc.scalar.copy, 1, half, PACK)
+        quant_we(0, 0, PACK)
+        quant_we(1, 0, half)
+        quant_x(0)
+        quant_we(1, half, PACK)
         for k in range(NC + 2):
             if live(k - 1):
                 relu_regroup(k - 1)
             if live(k - ACC_LAG):
                 accumulate(k - ACC_LAG)
             if k == NC + 1:
-                for c in range(k - ACC_LAG + 1, NC):
+                for c in range(k - ACC_LAG + 1, NC - 1):
                     accumulate(c)
             if live(k + 1):
                 transpose_x(k + 1)
-            if live(k - 2):
+            if live(k - 2) and vector_sums(k - 2):
                 sum_a(k - 2, 0, 2)
             if live(k - 1):
                 quant_h(k - 1)
             if live(k - 2):
                 back(k - 2)
+            if k == NC + 1:
+                accumulate(NC - 1)
             if k == 0:
                 prep_we2_regroup()
             if live(k):
@@ -341,19 +362,19 @@ def tile_bipartiteneuralmessagepassinglayer_pa_t_kernel(
             if live(k - 1):
                 for m in range(BLOCKS):
                     stage2(k - 1, m)
-            if live(k - 2):
+            if live(k - 2) and vector_sums(k - 2):
                 sum_a(k - 2, 2, VECTOR_SUM_BLOCKS)
 
         pa = bank("ps_suma")
         for m in range(BLOCKS):
             nc.tensor.transpose(pa[:, m * P : (m + 1) * P], st[:, m, :], ident[:])
-        so_a = const.tile([P, ED], F32, name="so_a")
-        nc.scalar.copy(out=so_a[:], in_=pa[:])
-        nc.sync.dma_start(out=out_1, in_=so_a[0:NA, :])
         acc_sb = const.tile([P, ED], F32, name="acc_sb")
+        so_a = const.tile([P, ED], F32, name="so_a")
+        so_b = const.tile([P, ED], F32, name="so_b")
         nc.vector.tensor_copy(out=acc_sb[:], in_=acc[:])
         pb = bank("ps_sumb")
         nc.tensor.matmul(out=pb[:], lhsT=sel[:], rhs=acc_sb[:], start=True, stop=True)
-        so_b = const.tile([P, ED], F32, name="so_b")
+        nc.scalar.copy(out=so_a[:], in_=pa[:])
+        nc.sync.dma_start(out=out_1, in_=so_a[0:NA, :])
         nc.vector.tensor_copy(out=so_b[:], in_=pb[:])
         nc.sync.dma_start(out=out_2, in_=so_b[0:NB, :])

@@ -53,15 +53,18 @@ def tile_bipartiteneuralmessagepassinglayer_pa_t_kernel(
             return psum.tile([P, BANK], F32, tag="bank", name=label)
 
         ab_bf = const.tile([P, ED], BF16, name="ab_bf")
-        bias_bf = const.tile([P, P], BF16, name="bias_bf")
         be1_bf = const.tile([P, PACK], BF16, name="be1_bf")
-        nc.vector.memset(bias_bf[:], 0.0)
-        nc.scalar.dma_start(out=ab_bf[0:NA, :], in_=a_proj)
-        nc.scalar.dma_start(out=ab_bf[NA:P, :], in_=b_proj)
-        nc.scalar.dma_start(out=be1_bf[:], in_=be1.rearrange("(p t) -> p t", t=PACK))
-        nc.scalar.dma_start(out=bias_bf[0:BLOCKS, :], in_=be2.rearrange("(m f) -> m f", m=BLOCKS))
+        be2_bf = const.tile([P, PACK], BF16, name="be2_bf")
+        nc.sync.dma_start(out=ab_bf[0:NA, :], in_=a_proj)
+        nc.sync.dma_start(out=ab_bf[NA:P, :], in_=b_proj)
+        nc.sync.dma_start(out=be1_bf[:], in_=be1.rearrange("(p t) -> p t", t=PACK))
+        warm = const.tile([P, 2], F32, name="warm")
+        nc.vector.memset(warm[:], 0.0)
+        nc.scalar.activation(out=warm[:, 1:2], in_=warm[:, 0:1], func=RELU)
         ident = const.tile([P, P], F32, name="ident")
         make_identity(nc, ident[:])
+        ident_bf = const.tile([P, P], BF16, name="ident_bf")
+        nc.vector.tensor_copy(out=ident_bf[:], in_=ident[:])
         acc = psacc.tile([P, ED], F32, name="acc")
 
         xs = const.tile([P, ALL_TILES, K1], BF16, name="xs")
@@ -76,19 +79,16 @@ def tile_bipartiteneuralmessagepassinglayer_pa_t_kernel(
             rows = We[g * P * PACK : (g + 1) * P * PACK, :]
             nc.sync.dma_start(out=wraw[:, g, :, :], in_=rows.rearrange("(p t) c -> p t c", t=PACK))
 
-        load_x(0)
         load_w(0)
+        load_x(0)
         load_w(1)
         load_x(2)
         load_x(4)
         nc.sync.dma_start(out=w2raw[:], in_=We2.rearrange("(p t) c -> p t c", t=PACK))
+        nc.sync.dma_start(out=be2_bf[:], in_=be2.rearrange("(p t) -> p t", t=PACK))
         for t in range(6, ALL_TILES, 2):
             load_x(t)
 
-        ab32 = const.tile([P, ED], F32, name="ab32")
-        bias32 = const.tile([P, P], F32, name="bias32")
-        be1T = const.tile([P, PACK], F32, name="be1T")
-        biasT = const.tile([P, BLOCKS], F32, name="biasT")
         abT = const.tile([P, PACK, P], F32, name="abT")
         st = const.tile([P, BLOCKS, P], F32, name="st")
         sel = const.tile([P, P], F32, name="sel")
@@ -98,32 +98,22 @@ def tile_bipartiteneuralmessagepassinglayer_pa_t_kernel(
                 out=sel[:, half * NB : (half + 1) * NB], in0=ident[:, 0:NB], in1=ident[:, NB:P], op=ADD
             )
 
-        def small_inputs_cast():
-            nc.scalar.copy(out=ab32[:], in_=ab_bf[:])
-            nc.scalar.copy(out=bias32[:], in_=bias_bf[:])
-            nc.scalar.copy(out=be1T[:], in_=be1_bf[:])
-
         def small_inputs_transpose():
-            ps_ab = bank("ps_ab")
+            ps_ab = psum.tile([P, PACK, P], BF16, tag="bank", name="ps_ab")
             for t in range(PACK):
-                nc.tensor.transpose(ps_ab[:, t * P : (t + 1) * P], ab32[:, t:ED:PACK], ident[:])
-            ps_bias = bank("ps_bias")
-            nc.tensor.transpose(ps_bias[:, 0:P], bias32[:], ident[:])
-            return ps_ab, ps_bias
+                nc.tensor.transpose(ps_ab[:, t, :], ab_bf[:, t:ED:PACK], ident_bf[:])
+            return ps_ab
 
-        def small_inputs_finish(ps_ab, ps_bias):
-            nc.scalar.copy(
-                out=abT[:, :, 0:NA], in_=ps_ab[:].rearrange("p (t r) -> p t r", t=PACK)[:, :, 0:NA]
-            )
+        def small_inputs_finish(ps_ab):
+            nc.scalar.copy(out=abT[:, :, 0:NA], in_=ps_ab[:, :, 0:NA])
             for t in range(PACK):
                 nc.scalar.activation(
                     out=abT[:, t, NA:P],
-                    in_=ps_ab[:, t * P + NA : (t + 1) * P],
+                    in_=ps_ab[:, t, NA:P],
                     func=IDENTITY,
-                    bias=be1T[:, t : t + 1],
+                    bias=be1_bf[:, t : t + 1],
                     scale=1.0,
                 )
-            nc.scalar.copy(out=biasT[:], in_=ps_bias[:, 0:BLOCKS])
 
         wg = const.tile([P, PASSES, ED, PACK], BF16, name="wg", align_bytes=64)
         wq = const.tile([P, PASSES * ED], U32, name="wq", align_bytes=64)
@@ -132,16 +122,10 @@ def tile_bipartiteneuralmessagepassinglayer_pa_t_kernel(
         w2q = const.tile([P, ED], U32, name="w2q", align_bytes=64)
         w2sc = const.tile([P, ED], U8, name="w2sc", align_bytes=64)
 
-        def regroup(eng_copy, dst, src):
+        def regroup(eng_copy, dst, src, t0, t1):
             eng_copy(
-                out=dst.rearrange("p (c z) t -> p c t z", z=4),
-                in_=src.rearrange("p t (c z) -> p c t z", z=4),
-            )
-
-        def regroup_we(eng_copy, g, t0, t1):
-            eng_copy(
-                out=wg[:, g, t0 * P : t1 * P, :].rearrange("p (t m) j -> p t m j", m=P),
-                in_=wraw[:, g, :, :].rearrange("p j (m t) -> p t m j", t=PACK)[:, t0:t1, :, :],
+                out=dst[:, t0 * P : t1 * P, :].rearrange("p (t m) j -> p t m j", m=P),
+                in_=src.rearrange("p j (m t) -> p t m j", t=PACK)[:, t0:t1, :, :],
             )
 
         def quant_we(g, t0, t1):
@@ -153,7 +137,7 @@ def tile_bipartiteneuralmessagepassinglayer_pa_t_kernel(
             )
 
         def prep_we2_regroup():
-            regroup(nc.scalar.copy, w2g[:], w2raw[:])
+            regroup(nc.scalar.copy, w2g, w2raw[:], 0, PACK)
 
         def prep_we2_quant():
             nc.vector.quantize_mx(
@@ -268,7 +252,7 @@ def tile_bipartiteneuralmessagepassinglayer_pa_t_kernel(
             )
             if m < vector_sums(c):
                 nc.scalar.activation(
-                    out=lt[c][:, m, :], in_=pb[:, 0:n], func=RELU, bias=biasT[:, m : m + 1], scale=1.0
+                    out=lt[c][:, m, :], in_=pb[:, 0:n], func=RELU, bias=be2_bf[:, m : m + 1], scale=1.0
                 )
             else:
                 for il in range(2 * TILES[c]):
@@ -277,10 +261,16 @@ def tile_bipartiteneuralmessagepassinglayer_pa_t_kernel(
                         out=lt[c][:, m, il * NB : (il + 1) * NB],
                         in_=pb[:, il * NB : (il + 1) * NB],
                         func=RELU,
-                        bias=biasT[:, m : m + 1],
+                        bias=be2_bf[:, m : m + 1],
                         scale=1.0,
                         accum_out=st[:, m, i : i + 1],
                     )
+
+        def in_blocks(pb):
+            return pb[:].rearrange("e (m p) -> e p m", m=BLOCKS)
+
+        def rows_of(sb):
+            return sb.rearrange("e (p m) -> e p m", m=BLOCKS)
 
         def sum_a(c, m0, m1):
             i0 = 2 * first_tile[c]
@@ -301,7 +291,7 @@ def tile_bipartiteneuralmessagepassinglayer_pa_t_kernel(
                         pb[:, m * P : (m + 1) * P], lt[c][:, m, tl * P : (tl + 1) * P], ident[:]
                     )
                 back_copy = nc.scalar.copy if c < NC - LAST else nc.vector.tensor_copy
-                back_copy(out=lo[c][:, tl, :], in_=pb[:])
+                back_copy(out=rows_of(lo[c][:, tl, :]), in_=in_blocks(pb))
                 if c == NC - 1:
                     nc.sync.dma_start(out=o_rows[r0 + tl * P : r0 + (tl + 1) * P, :], in_=lo[c][:, tl, :])
             if c < NC - 1:
@@ -321,16 +311,15 @@ def tile_bipartiteneuralmessagepassinglayer_pa_t_kernel(
                     )
 
         half = PACK // 2
-        small_inputs_cast()
         transpose_x(0)
-        ps_small = small_inputs_transpose()
-        small_inputs_finish(ps_small[0], ps_small[1])
-        regroup_we(nc.vector.tensor_copy, 0, 0, PACK)
-        regroup_we(nc.vector.tensor_copy, 1, 0, half)
-        regroup_we(nc.scalar.copy, 1, half, PACK)
+        ps_ab = small_inputs_transpose()
+        small_inputs_finish(ps_ab)
+        regroup(nc.vector.tensor_copy, wg[:, 0, :, :], wraw[:, 0, :, :], 0, PACK)
         quant_we(0, 0, PACK)
-        quant_we(1, 0, half)
+        regroup(nc.vector.tensor_copy, wg[:, 1, :, :], wraw[:, 1, :, :], 0, half)
         quant_x(0)
+        quant_we(1, 0, half)
+        regroup(nc.vector.tensor_copy, wg[:, 1, :, :], wraw[:, 1, :, :], half, PACK)
         quant_we(1, half, PACK)
         for k in range(NC + 2):
             if live(k - 1):
@@ -371,10 +360,10 @@ def tile_bipartiteneuralmessagepassinglayer_pa_t_kernel(
         acc_sb = const.tile([P, ED], F32, name="acc_sb")
         so_a = const.tile([P, ED], F32, name="so_a")
         so_b = const.tile([P, ED], F32, name="so_b")
-        nc.vector.tensor_copy(out=acc_sb[:], in_=acc[:])
+        nc.vector.tensor_copy(out=rows_of(acc_sb[:]), in_=in_blocks(acc))
         pb = bank("ps_sumb")
         nc.tensor.matmul(out=pb[:], lhsT=sel[:], rhs=acc_sb[:], start=True, stop=True)
-        nc.scalar.copy(out=so_a[:], in_=pa[:])
+        nc.scalar.copy(out=rows_of(so_a[:]), in_=in_blocks(pa))
         nc.sync.dma_start(out=out_1, in_=so_a[0:NA, :])
         nc.vector.tensor_copy(out=so_b[:], in_=pb[:])
         nc.sync.dma_start(out=out_2, in_=so_b[0:NB, :])

@@ -27,7 +27,7 @@ PAIR = 2 * P
 FLOPS = 2 * NA * NB * K1 * ED + 2 * NA * NB * ED * ED
 
 TILES = (2, 2, 4, 4, 4, 4, 4, 4, 2, 2)
-VECTOR_SUM_BLOCKS = 3
+VECTOR_SUM_BLOCKS = 2
 LAST = 2
 ACC_LAG = 3
 
@@ -54,10 +54,12 @@ def tile_bipartiteneuralmessagepassinglayer_pa_t_kernel(
 
         ab_bf = const.tile([P, ED], BF16, name="ab_bf")
         be1_bf = const.tile([P, PACK], BF16, name="be1_bf")
-        be2_bf = const.tile([P, PACK], BF16, name="be2_bf")
+        be2_bf = const.tile([P, P], BF16, name="be2_bf")
+        nc.vector.memset(be2_bf[:], 0.0)
         nc.sync.dma_start(out=ab_bf[0:NA, :], in_=a_proj)
         nc.sync.dma_start(out=ab_bf[NA:P, :], in_=b_proj)
         nc.sync.dma_start(out=be1_bf[:], in_=be1.rearrange("(p t) -> p t", t=PACK))
+        nc.sync.dma_start(out=be2_bf[0:BLOCKS, :], in_=be2.rearrange("(m f) -> m f", m=BLOCKS))
         warm = const.tile([P, 2], F32, name="warm")
         nc.vector.memset(warm[:], 0.0)
         nc.scalar.activation(out=warm[:, 1:2], in_=warm[:, 0:1], func=RELU)
@@ -85,11 +87,11 @@ def tile_bipartiteneuralmessagepassinglayer_pa_t_kernel(
         load_x(2)
         load_x(4)
         nc.sync.dma_start(out=w2raw[:], in_=We2.rearrange("(p t) c -> p t c", t=PACK))
-        nc.sync.dma_start(out=be2_bf[:], in_=be2.rearrange("(p t) -> p t", t=PACK))
         for t in range(6, ALL_TILES, 2):
             load_x(t)
 
         abT = const.tile([P, PACK, P], F32, name="abT")
+        be2T = const.tile([P, BLOCKS], F32, name="be2T")
         st = const.tile([P, BLOCKS, P], F32, name="st")
         sel = const.tile([P, P], F32, name="sel")
         nc.gpsimd.memset(st[:], 0.0)
@@ -102,9 +104,11 @@ def tile_bipartiteneuralmessagepassinglayer_pa_t_kernel(
             ps_ab = psum.tile([P, PACK, P], BF16, tag="bank", name="ps_ab")
             for t in range(PACK):
                 nc.tensor.transpose(ps_ab[:, t, :], ab_bf[:, t:ED:PACK], ident_bf[:])
-            return ps_ab
+            ps_be2 = psum.tile([P, P], BF16, tag="bank", name="ps_be2")
+            nc.tensor.transpose(ps_be2[:], be2_bf[:], ident_bf[:])
+            return ps_ab, ps_be2
 
-        def small_inputs_finish(ps_ab):
+        def small_inputs_finish(ps_ab, ps_be2):
             nc.scalar.copy(out=abT[:, :, 0:NA], in_=ps_ab[:, :, 0:NA])
             for t in range(PACK):
                 nc.scalar.activation(
@@ -114,6 +118,7 @@ def tile_bipartiteneuralmessagepassinglayer_pa_t_kernel(
                     bias=be1_bf[:, t : t + 1],
                     scale=1.0,
                 )
+            nc.scalar.copy(out=be2T[:], in_=ps_be2[:, 0:BLOCKS])
 
         wg = const.tile([P, PASSES, ED, PACK], BF16, name="wg", align_bytes=64)
         wq = const.tile([P, PASSES * ED], U32, name="wq", align_bytes=64)
@@ -137,7 +142,10 @@ def tile_bipartiteneuralmessagepassinglayer_pa_t_kernel(
             )
 
         def prep_we2_regroup():
-            regroup(nc.scalar.copy, w2g, w2raw[:], 0, PACK)
+            nc.scalar.copy(
+                out=w2g[:].rearrange("p (c z) t -> p c t z", z=4),
+                in_=w2raw[:].rearrange("p t (c z) -> p c t z", z=4),
+            )
 
         def prep_we2_quant():
             nc.vector.quantize_mx(
@@ -152,6 +160,7 @@ def tile_bipartiteneuralmessagepassinglayer_pa_t_kernel(
         hq = {}
         hsc = {}
         lt = {}
+        ls = {}
         lo = {}
 
         def live(c):
@@ -252,7 +261,7 @@ def tile_bipartiteneuralmessagepassinglayer_pa_t_kernel(
             )
             if m < vector_sums(c):
                 nc.scalar.activation(
-                    out=lt[c][:, m, :], in_=pb[:, 0:n], func=RELU, bias=be2_bf[:, m : m + 1], scale=1.0
+                    out=lt[c][:, m, :], in_=pb[:, 0:n], func=RELU, bias=be2T[:, m : m + 1], scale=1.0
                 )
             else:
                 for il in range(2 * TILES[c]):
@@ -261,16 +270,10 @@ def tile_bipartiteneuralmessagepassinglayer_pa_t_kernel(
                         out=lt[c][:, m, il * NB : (il + 1) * NB],
                         in_=pb[:, il * NB : (il + 1) * NB],
                         func=RELU,
-                        bias=be2_bf[:, m : m + 1],
+                        bias=be2T[:, m : m + 1],
                         scale=1.0,
                         accum_out=st[:, m, i : i + 1],
                     )
-
-        def in_blocks(pb):
-            return pb[:].rearrange("e (m p) -> e p m", m=BLOCKS)
-
-        def rows_of(sb):
-            return sb.rearrange("e (p m) -> e p m", m=BLOCKS)
 
         def sum_a(c, m0, m1):
             i0 = 2 * first_tile[c]
@@ -291,29 +294,46 @@ def tile_bipartiteneuralmessagepassinglayer_pa_t_kernel(
                         pb[:, m * P : (m + 1) * P], lt[c][:, m, tl * P : (tl + 1) * P], ident[:]
                     )
                 back_copy = nc.scalar.copy if c < NC - LAST else nc.vector.tensor_copy
-                back_copy(out=rows_of(lo[c][:, tl, :]), in_=in_blocks(pb))
+                back_copy(out=lo[c][:, tl, :], in_=pb[:])
                 if c == NC - 1:
                     nc.sync.dma_start(out=o_rows[r0 + tl * P : r0 + (tl + 1) * P, :], in_=lo[c][:, tl, :])
             if c < NC - 1:
                 rows = o_rows[r0 : r0 + TILES[c] * P, :]
                 nc.sync.dma_start(out=rows.rearrange("(t p) f -> p t f", p=P), in_=lo[c][:])
 
+        def add_tiles(c):
+            half = work.tile([P, BLOCKS, PAIR], F32, name="lh%d" % c, tag="lh")
+            ls[c] = work.tile([P, BLOCKS, P], F32, name="ls%d" % c, tag="ls")
+            for m in range(BLOCKS):
+                nc.gpsimd.tensor_tensor(
+                    out=half[:, m, :], in0=lt[c][:, m, 0:PAIR], in1=lt[c][:, m, PAIR : 2 * PAIR], op=ADD
+                )
+            for m in range(0, BLOCKS, 2):
+                nc.gpsimd.tensor_tensor(
+                    out=ls[c][:, m : m + 2, :], in0=half[:, m : m + 2, 0:P], in1=half[:, m : m + 2, P:PAIR], op=ADD
+                )
+
+        def added(c):
+            return TILES[c] == 4
+
         def accumulate(c):
-            for tl in range(TILES[c]):
+            src = ls[c] if added(c) else lt[c]
+            tiles = 1 if added(c) else TILES[c]
+            for tl in range(tiles):
                 for m in range(BLOCKS):
                     nc.tensor.matmul(
                         out=acc[:, m * P : (m + 1) * P],
-                        lhsT=lt[c][:, m, tl * P : (tl + 1) * P],
+                        lhsT=src[:, m, tl * P : (tl + 1) * P],
                         rhs=ident[:],
                         is_transpose=True,
                         start=(c == 0 and tl == 0 and m == 0),
-                        stop=(c == NC - 1 and tl == TILES[c] - 1 and m == BLOCKS - 1),
+                        stop=(c == NC - 1 and tl == tiles - 1 and m == BLOCKS - 1),
                     )
 
         half = PACK // 2
         transpose_x(0)
-        ps_ab = small_inputs_transpose()
-        small_inputs_finish(ps_ab)
+        ps_ab, ps_be2 = small_inputs_transpose()
+        small_inputs_finish(ps_ab, ps_be2)
         regroup(nc.vector.tensor_copy, wg[:, 0, :, :], wraw[:, 0, :, :], 0, PACK)
         quant_we(0, 0, PACK)
         regroup(nc.vector.tensor_copy, wg[:, 1, :, :], wraw[:, 1, :, :], 0, half)
@@ -332,11 +352,13 @@ def tile_bipartiteneuralmessagepassinglayer_pa_t_kernel(
             if live(k + 1):
                 transpose_x(k + 1)
             if live(k - 2) and vector_sums(k - 2):
-                sum_a(k - 2, 0, 2)
+                sum_a(k - 2, 0, min(2, VECTOR_SUM_BLOCKS))
             if live(k - 1):
                 quant_h(k - 1)
             if live(k - 2):
                 back(k - 2)
+                if added(k - 2):
+                    add_tiles(k - 2)
             if k == NC + 1:
                 accumulate(NC - 1)
             if k == 0:
@@ -351,7 +373,7 @@ def tile_bipartiteneuralmessagepassinglayer_pa_t_kernel(
             if live(k - 1):
                 for m in range(BLOCKS):
                     stage2(k - 1, m)
-            if live(k - 2) and vector_sums(k - 2):
+            if live(k - 2) and vector_sums(k - 2) > 2:
                 sum_a(k - 2, 2, VECTOR_SUM_BLOCKS)
 
         pa = bank("ps_suma")
@@ -360,10 +382,10 @@ def tile_bipartiteneuralmessagepassinglayer_pa_t_kernel(
         acc_sb = const.tile([P, ED], F32, name="acc_sb")
         so_a = const.tile([P, ED], F32, name="so_a")
         so_b = const.tile([P, ED], F32, name="so_b")
-        nc.vector.tensor_copy(out=rows_of(acc_sb[:]), in_=in_blocks(acc))
+        nc.vector.tensor_copy(out=acc_sb[:], in_=acc[:])
         pb = bank("ps_sumb")
         nc.tensor.matmul(out=pb[:], lhsT=sel[:], rhs=acc_sb[:], start=True, stop=True)
-        nc.scalar.copy(out=rows_of(so_a[:]), in_=in_blocks(pa))
+        nc.scalar.copy(out=so_a[:], in_=pa[:])
         nc.sync.dma_start(out=out_1, in_=so_a[0:NA, :])
         nc.vector.tensor_copy(out=so_b[:], in_=pb[:])
         nc.sync.dma_start(out=out_2, in_=so_b[0:NB, :])

@@ -8,6 +8,7 @@ BF16 = mybir.dt.bfloat16
 U32 = mybir.dt.uint32
 U8 = mybir.dt.uint8
 FP8X4 = mybir.dt.float8_e4m3fn_x4
+MAX = mybir.AluOpType.max
 ADD = mybir.AluOpType.add
 AX_X = mybir.AxisListType.X
 RELU = mybir.ActivationFunctionType.Relu
@@ -27,8 +28,10 @@ PAIR = 2 * P
 FLOPS = 2 * NA * NB * K1 * ED + 2 * NA * NB * ED * ED
 
 TILES = (2, 2, 4, 4, 4, 4, 4, 4, 2, 2)
-VECTOR_SUM_BLOCKS = 2
+VECTOR_SUM_BLOCKS = 3
 LAST = 2
+SPLIT = 2
+SPLIT_SCALAR = 1
 ACC_LAG = 3
 
 
@@ -152,6 +155,7 @@ def tile_bipartiteneuralmessagepassinglayer_pa_t_kernel(
                 out=w2q[:].bitcast(FP8X4), scales=w2sc[:], in_=w2g[:].rearrange("p c t -> p (c t)")
             )
 
+        xp = {}
         xg = {}
         xq = {}
         xsc = {}
@@ -160,7 +164,6 @@ def tile_bipartiteneuralmessagepassinglayer_pa_t_kernel(
         hq = {}
         hsc = {}
         lt = {}
-        ls = {}
         lo = {}
 
         def live(c):
@@ -168,6 +171,26 @@ def tile_bipartiteneuralmessagepassinglayer_pa_t_kernel(
 
         def vector_sums(c):
             return VECTOR_SUM_BLOCKS if c < NC - LAST else 0
+
+        def splits(c):
+            return SPLIT if TILES[c] == 4 else 0
+
+        def split_words(c):
+            t0 = first_tile[c]
+            n = splits(c)
+            xp[c] = work.tile([P, n, PASSES, 2, P], F32, name="xp%d" % c, tag="xp", align_bytes=64)
+            for copy, a, b in ((nc.vector.tensor_copy, 0, n - SPLIT_SCALAR), (nc.scalar.copy, n - SPLIT_SCALAR, n)):
+                if a < b:
+                    copy(
+                        out=xp[c][:, a:b, :, :, :].rearrange("p t g u w -> p (t g) u w"),
+                        in_=xs[:, t0 + a : t0 + b, :].bitcast(F32).rearrange("p t (g w u) -> p (t g) u w", g=PASSES, u=2),
+                    )
+
+        def x_words(c, tl, g, u):
+            if tl < splits(c):
+                return xp[c][:, tl, g, u, :]
+            words = xs[:, first_tile[c] + tl, :].bitcast(F32)
+            return words[:, 2 * P * g + u : 2 * P * (g + 1) : 2]
 
         def transpose_x(c):
             n = TILES[c] * P
@@ -177,10 +200,9 @@ def tile_bipartiteneuralmessagepassinglayer_pa_t_kernel(
                     pb = bank("xt%d_%d_%d" % (c, g, pair))
                     for u in range(2):
                         for side in range(2):
-                            words = xs[:, first_tile[c] + 2 * pair + side, :].bitcast(F32)
                             nc.tensor.transpose(
                                 pb[:, u * PAIR + side * P : u * PAIR + (side + 1) * P],
-                                words[:, 2 * P * g + u : 2 * P * (g + 1) : 2],
+                                x_words(c, 2 * pair + side, g, u),
                                 ident[:],
                             )
                     nc.scalar.copy(
@@ -259,7 +281,16 @@ def tile_bipartiteneuralmessagepassinglayer_pa_t_kernel(
                 start=True,
                 stop=True,
             )
-            if m < vector_sums(c):
+            if c == NC - 1 and m % 2 == 1:
+                nc.vector.tensor_scalar(
+                    out=lt[c][:, m, :],
+                    in0=pb[:, 0:n],
+                    scalar1=be2T[:, m : m + 1],
+                    scalar2=0.0,
+                    op0=ADD,
+                    op1=MAX,
+                )
+            elif m < vector_sums(c):
                 nc.scalar.activation(
                     out=lt[c][:, m, :], in_=pb[:, 0:n], func=RELU, bias=be2T[:, m : m + 1], scale=1.0
                 )
@@ -275,11 +306,11 @@ def tile_bipartiteneuralmessagepassinglayer_pa_t_kernel(
                         accum_out=st[:, m, i : i + 1],
                     )
 
-        def sum_a(c, m0, m1):
+        def sum_a(c, m0, m1, step=1):
             i0 = 2 * first_tile[c]
             nc.vector.tensor_reduce(
-                out=st[:, m0:m1, i0 : i0 + 2 * TILES[c]],
-                in_=lt[c][:, m0:m1, :].rearrange("p m (i j) -> p m i j", j=NB),
+                out=st[:, m0:m1:step, i0 : i0 + 2 * TILES[c]],
+                in_=lt[c][:, m0:m1:step, :].rearrange("p m (i j) -> p m i j", j=NB),
                 axis=AX_X,
                 op=ADD,
             )
@@ -293,7 +324,7 @@ def tile_bipartiteneuralmessagepassinglayer_pa_t_kernel(
                     nc.tensor.transpose(
                         pb[:, m * P : (m + 1) * P], lt[c][:, m, tl * P : (tl + 1) * P], ident[:]
                     )
-                back_copy = nc.scalar.copy if c < NC - LAST else nc.vector.tensor_copy
+                back_copy = nc.vector.tensor_copy if c >= NC - LAST and tl % 2 == 1 else nc.scalar.copy
                 back_copy(out=lo[c][:, tl, :], in_=pb[:])
                 if c == NC - 1:
                     nc.sync.dma_start(out=o_rows[r0 + tl * P : r0 + (tl + 1) * P, :], in_=lo[c][:, tl, :])
@@ -301,33 +332,16 @@ def tile_bipartiteneuralmessagepassinglayer_pa_t_kernel(
                 rows = o_rows[r0 : r0 + TILES[c] * P, :]
                 nc.sync.dma_start(out=rows.rearrange("(t p) f -> p t f", p=P), in_=lo[c][:])
 
-        def add_tiles(c):
-            half = work.tile([P, BLOCKS, PAIR], F32, name="lh%d" % c, tag="lh")
-            ls[c] = work.tile([P, BLOCKS, P], F32, name="ls%d" % c, tag="ls")
-            for m in range(BLOCKS):
-                nc.gpsimd.tensor_tensor(
-                    out=half[:, m, :], in0=lt[c][:, m, 0:PAIR], in1=lt[c][:, m, PAIR : 2 * PAIR], op=ADD
-                )
-            for m in range(0, BLOCKS, 2):
-                nc.gpsimd.tensor_tensor(
-                    out=ls[c][:, m : m + 2, :], in0=half[:, m : m + 2, 0:P], in1=half[:, m : m + 2, P:PAIR], op=ADD
-                )
-
-        def added(c):
-            return TILES[c] == 4
-
         def accumulate(c):
-            src = ls[c] if added(c) else lt[c]
-            tiles = 1 if added(c) else TILES[c]
-            for tl in range(tiles):
+            for tl in range(TILES[c]):
                 for m in range(BLOCKS):
                     nc.tensor.matmul(
                         out=acc[:, m * P : (m + 1) * P],
-                        lhsT=src[:, m, tl * P : (tl + 1) * P],
+                        lhsT=lt[c][:, m, tl * P : (tl + 1) * P],
                         rhs=ident[:],
                         is_transpose=True,
                         start=(c == 0 and tl == 0 and m == 0),
-                        stop=(c == NC - 1 and tl == tiles - 1 and m == BLOCKS - 1),
+                        stop=(c == NC - 1 and tl == TILES[c] - 1 and m == BLOCKS - 1),
                     )
 
         half = PACK // 2
@@ -352,13 +366,13 @@ def tile_bipartiteneuralmessagepassinglayer_pa_t_kernel(
             if live(k + 1):
                 transpose_x(k + 1)
             if live(k - 2) and vector_sums(k - 2):
-                sum_a(k - 2, 0, min(2, VECTOR_SUM_BLOCKS))
+                sum_a(k - 2, 0, VECTOR_SUM_BLOCKS if k == NC - 1 else 2)
             if live(k - 1):
                 quant_h(k - 1)
             if live(k - 2):
                 back(k - 2)
-                if added(k - 2):
-                    add_tiles(k - 2)
+            if live(k + 2) and splits(k + 2):
+                split_words(k + 2)
             if k == NC + 1:
                 accumulate(NC - 1)
             if k == 0:
@@ -373,7 +387,9 @@ def tile_bipartiteneuralmessagepassinglayer_pa_t_kernel(
             if live(k - 1):
                 for m in range(BLOCKS):
                     stage2(k - 1, m)
-            if live(k - 2) and vector_sums(k - 2) > 2:
+            if k == NC:
+                sum_a(NC - 1, 1, BLOCKS, 2)
+            if live(k - 2) and vector_sums(k - 2) and k < NC - 1:
                 sum_a(k - 2, 2, VECTOR_SUM_BLOCKS)
 
         pa = bank("ps_suma")

@@ -31,6 +31,7 @@ TILES = (2, 2, 4, 4, 4, 4, 4, 4, 2, 2)
 VECTOR_SUM_BLOCKS = 3
 LAST = 2
 SPLIT = 2
+WARM_UP_PASSES = 8
 SPLIT_SCALAR = 1
 ACC_LAG = 3
 
@@ -71,6 +72,11 @@ def tile_bipartiteneuralmessagepassinglayer_pa_t_kernel(
         ident_bf = const.tile([P, P], BF16, name="ident_bf")
         nc.vector.tensor_copy(out=ident_bf[:], in_=ident[:])
         acc = psacc.tile([P, ED], F32, name="acc")
+        zeros = const.tile([P, BANK], BF16, name="zeros")
+        nc.vector.memset(zeros[:], 0.0)
+        idle = bank("idle")
+        for n in range(WARM_UP_PASSES):
+            nc.tensor.matmul(out=idle[:], lhsT=zeros[:, 0:P], rhs=zeros[:], start=True, stop=True)
 
         xs = const.tile([P, ALL_TILES, K1], BF16, name="xs")
         wraw = const.tile([P, PASSES, PACK, ED], BF16, name="wraw")
@@ -361,7 +367,7 @@ def tile_bipartiteneuralmessagepassinglayer_pa_t_kernel(
             if live(k - ACC_LAG):
                 accumulate(k - ACC_LAG)
             if k == NC + 1:
-                for c in range(k - ACC_LAG + 1, NC - 1):
+                for c in range(k - ACC_LAG + 1, NC):
                     accumulate(c)
             if live(k + 1):
                 transpose_x(k + 1)
@@ -369,12 +375,10 @@ def tile_bipartiteneuralmessagepassinglayer_pa_t_kernel(
                 sum_a(k - 2, 0, VECTOR_SUM_BLOCKS if k == NC - 1 else 2)
             if live(k - 1):
                 quant_h(k - 1)
-            if live(k - 2):
+            if live(k - 2) and k < NC + 1:
                 back(k - 2)
             if live(k + 2) and splits(k + 2):
                 split_words(k + 2)
-            if k == NC + 1:
-                accumulate(NC - 1)
             if k == 0:
                 prep_we2_regroup()
             if live(k):
@@ -392,16 +396,21 @@ def tile_bipartiteneuralmessagepassinglayer_pa_t_kernel(
             if live(k - 2) and vector_sums(k - 2) and k < NC - 1:
                 sum_a(k - 2, 2, VECTOR_SUM_BLOCKS)
 
-        pa = bank("ps_suma")
-        for m in range(BLOCKS):
-            nc.tensor.transpose(pa[:, m * P : (m + 1) * P], st[:, m, :], ident[:])
         acc_sb = const.tile([P, ED], F32, name="acc_sb")
         so_a = const.tile([P, ED], F32, name="so_a")
         so_b = const.tile([P, ED], F32, name="so_b")
-        nc.vector.tensor_copy(out=acc_sb[:], in_=acc[:])
-        pb = bank("ps_sumb")
-        nc.tensor.matmul(out=pb[:], lhsT=sel[:], rhs=acc_sb[:], start=True, stop=True)
-        nc.scalar.copy(out=so_a[:], in_=pa[:])
-        nc.sync.dma_start(out=out_1, in_=so_a[0:NA, :])
-        nc.vector.tensor_copy(out=so_b[:], in_=pb[:])
+        lo_half = slice(0, ED // 2)
+        hi_half = slice(ED // 2, ED)
+        nc.vector.tensor_copy(out=acc_sb[:, lo_half], in_=acc[:, lo_half])
+        nc.vector.tensor_copy(out=acc_sb[:, hi_half], in_=acc[:, hi_half])
+        back(NC - 1)
+        pa = bank("ps_suma")
+        for m in range(BLOCKS):
+            nc.tensor.transpose(pa[:, m * P : (m + 1) * P], st[:, m, :], ident[:])
+        for cols in (lo_half, hi_half):
+            pb = bank("ps_sumb")
+            nc.tensor.matmul(out=pb[:, cols], lhsT=sel[:], rhs=acc_sb[:, cols], start=True, stop=True)
+            nc.vector.tensor_copy(out=so_b[:, cols], in_=pb[:, cols])
         nc.sync.dma_start(out=out_2, in_=so_b[0:NB, :])
+        nc.scalar.copy(out=so_a[:], in_=pa[:])
+        nc.scalar.dma_start(out=out_1, in_=so_a[0:NA, :])

@@ -30,8 +30,8 @@ FLOPS = 2 * NA * NB * K1 * ED + 2 * NA * NB * ED * ED
 TILES = (2, 2, 4, 4, 4, 4, 4, 4, 2, 2)
 VECTOR_SUM_BLOCKS = 3
 LAST = 2
-SPLIT = 2
-WARM_UP_PASSES = 8
+SPLIT = 3
+SPLIT_FROM = 3
 SPLIT_SCALAR = 1
 ACC_LAG = 3
 
@@ -60,23 +60,23 @@ def tile_bipartiteneuralmessagepassinglayer_pa_t_kernel(
         be1_bf = const.tile([P, PACK], BF16, name="be1_bf")
         be2_bf = const.tile([P, P], BF16, name="be2_bf")
         nc.vector.memset(be2_bf[:], 0.0)
-        nc.sync.dma_start(out=ab_bf[0:NA, :], in_=a_proj)
-        nc.sync.dma_start(out=ab_bf[NA:P, :], in_=b_proj)
-        nc.sync.dma_start(out=be1_bf[:], in_=be1.rearrange("(p t) -> p t", t=PACK))
-        nc.sync.dma_start(out=be2_bf[0:BLOCKS, :], in_=be2.rearrange("(m f) -> m f", m=BLOCKS))
         warm = const.tile([P, 2], F32, name="warm")
         nc.vector.memset(warm[:], 0.0)
         nc.scalar.activation(out=warm[:, 1:2], in_=warm[:, 0:1], func=RELU)
+        zeros = const.tile([P, BANK], BF16, name="zeros")
+        nc.vector.memset(zeros[:], 0.0)
         ident = const.tile([P, P], F32, name="ident")
         make_identity(nc, ident[:])
         ident_bf = const.tile([P, P], BF16, name="ident_bf")
         nc.vector.tensor_copy(out=ident_bf[:], in_=ident[:])
         acc = psacc.tile([P, ED], F32, name="acc")
-        zeros = const.tile([P, BANK], BF16, name="zeros")
-        nc.vector.memset(zeros[:], 0.0)
         idle = bank("idle")
-        for n in range(WARM_UP_PASSES):
-            nc.tensor.matmul(out=idle[:], lhsT=zeros[:, 0:P], rhs=zeros[:], start=True, stop=True)
+
+        def warm_up(passes):
+            for n in range(passes):
+                nc.tensor.matmul(out=idle[:], lhsT=zeros[:, 0:P], rhs=zeros[:], start=True, stop=True)
+
+        warm_up(8)
 
         xs = const.tile([P, ALL_TILES, K1], BF16, name="xs")
         wraw = const.tile([P, PASSES, PACK, ED], BF16, name="wraw")
@@ -93,8 +93,12 @@ def tile_bipartiteneuralmessagepassinglayer_pa_t_kernel(
         load_w(0)
         load_x(0)
         load_w(1)
+        nc.sync.dma_start(out=ab_bf[0:NA, :], in_=a_proj)
+        nc.sync.dma_start(out=ab_bf[NA:P, :], in_=b_proj)
+        nc.sync.dma_start(out=be1_bf[:], in_=be1.rearrange("(p t) -> p t", t=PACK))
         load_x(2)
         load_x(4)
+        nc.sync.dma_start(out=be2_bf[0:BLOCKS, :], in_=be2.rearrange("(m f) -> m f", m=BLOCKS))
         nc.sync.dma_start(out=w2raw[:], in_=We2.rearrange("(p t) c -> p t c", t=PACK))
         for t in range(6, ALL_TILES, 2):
             load_x(t)
@@ -113,11 +117,9 @@ def tile_bipartiteneuralmessagepassinglayer_pa_t_kernel(
             ps_ab = psum.tile([P, PACK, P], BF16, tag="bank", name="ps_ab")
             for t in range(PACK):
                 nc.tensor.transpose(ps_ab[:, t, :], ab_bf[:, t:ED:PACK], ident_bf[:])
-            ps_be2 = psum.tile([P, P], BF16, tag="bank", name="ps_be2")
-            nc.tensor.transpose(ps_be2[:], be2_bf[:], ident_bf[:])
-            return ps_ab, ps_be2
+            return ps_ab
 
-        def small_inputs_finish(ps_ab, ps_be2):
+        def small_inputs_finish(ps_ab):
             nc.scalar.copy(out=abT[:, :, 0:NA], in_=ps_ab[:, :, 0:NA])
             for t in range(PACK):
                 nc.scalar.activation(
@@ -127,6 +129,10 @@ def tile_bipartiteneuralmessagepassinglayer_pa_t_kernel(
                     bias=be1_bf[:, t : t + 1],
                     scale=1.0,
                 )
+
+        def be2_columns():
+            ps_be2 = psum.tile([P, P], BF16, tag="bank", name="ps_be2")
+            nc.tensor.transpose(ps_be2[:], be2_bf[:], ident_bf[:])
             nc.scalar.copy(out=be2T[:], in_=ps_be2[:, 0:BLOCKS])
 
         wg = const.tile([P, PASSES, ED, PACK], BF16, name="wg", align_bytes=64)
@@ -179,7 +185,7 @@ def tile_bipartiteneuralmessagepassinglayer_pa_t_kernel(
             return VECTOR_SUM_BLOCKS if c < NC - LAST else 0
 
         def splits(c):
-            return SPLIT if TILES[c] == 4 else 0
+            return SPLIT if TILES[c] == 4 and c >= SPLIT_FROM else 0
 
         def split_words(c):
             t0 = first_tile[c]
@@ -352,8 +358,9 @@ def tile_bipartiteneuralmessagepassinglayer_pa_t_kernel(
 
         half = PACK // 2
         transpose_x(0)
-        ps_ab, ps_be2 = small_inputs_transpose()
-        small_inputs_finish(ps_ab, ps_be2)
+        ps_ab = small_inputs_transpose()
+        small_inputs_finish(ps_ab)
+        warm_up(2)
         regroup(nc.vector.tensor_copy, wg[:, 0, :, :], wraw[:, 0, :, :], 0, PACK)
         quant_we(0, 0, PACK)
         regroup(nc.vector.tensor_copy, wg[:, 1, :, :], wraw[:, 1, :, :], 0, half)
@@ -387,6 +394,7 @@ def tile_bipartiteneuralmessagepassinglayer_pa_t_kernel(
             if live(k + 1):
                 quant_x(k + 1)
             if k == 0:
+                be2_columns()
                 prep_we2_quant()
             if live(k - 1):
                 for m in range(BLOCKS):

@@ -32,6 +32,7 @@ VECTOR_SUM_BLOCKS = 3
 LAST = 2
 SPLIT = 3
 SPLIT_FROM = 3
+SPLIT_SHORT = 1
 SPLIT_SCALAR = 1
 ACC_LAG = 3
 
@@ -185,18 +186,19 @@ def tile_bipartiteneuralmessagepassinglayer_pa_t_kernel(
             return VECTOR_SUM_BLOCKS if c < NC - LAST else 0
 
         def splits(c):
-            return SPLIT if TILES[c] == 4 and c >= SPLIT_FROM else 0
+            if c < SPLIT_FROM:
+                return 0
+            return SPLIT if TILES[c] == 4 else SPLIT_SHORT
 
-        def split_words(c):
+        def split_words(c, copy, a, b):
             t0 = first_tile[c]
-            n = splits(c)
-            xp[c] = work.tile([P, n, PASSES, 2, P], F32, name="xp%d" % c, tag="xp", align_bytes=64)
-            for copy, a, b in ((nc.vector.tensor_copy, 0, n - SPLIT_SCALAR), (nc.scalar.copy, n - SPLIT_SCALAR, n)):
-                if a < b:
-                    copy(
-                        out=xp[c][:, a:b, :, :, :].rearrange("p t g u w -> p (t g) u w"),
-                        in_=xs[:, t0 + a : t0 + b, :].bitcast(F32).rearrange("p t (g w u) -> p (t g) u w", g=PASSES, u=2),
-                    )
+            if c not in xp:
+                xp[c] = work.tile([P, splits(c), PASSES, 2, P], F32, name="xp%d" % c, tag="xp", align_bytes=64)
+            if a < b:
+                copy(
+                    out=xp[c][:, a:b, :, :, :].rearrange("p t g u w -> p (t g) u w"),
+                    in_=xs[:, t0 + a : t0 + b, :].bitcast(F32).rearrange("p t (g w u) -> p (t g) u w", g=PASSES, u=2),
+                )
 
         def x_words(c, tl, g, u):
             if tl < splits(c):
@@ -364,9 +366,9 @@ def tile_bipartiteneuralmessagepassinglayer_pa_t_kernel(
         regroup(nc.vector.tensor_copy, wg[:, 0, :, :], wraw[:, 0, :, :], 0, PACK)
         quant_we(0, 0, PACK)
         regroup(nc.vector.tensor_copy, wg[:, 1, :, :], wraw[:, 1, :, :], 0, half)
+        regroup(nc.vector.tensor_copy, wg[:, 1, :, :], wraw[:, 1, :, :], half, PACK)
         quant_x(0)
         quant_we(1, 0, half)
-        regroup(nc.vector.tensor_copy, wg[:, 1, :, :], wraw[:, 1, :, :], half, PACK)
         quant_we(1, half, PACK)
         for k in range(NC + 2):
             if live(k - 1):
@@ -380,12 +382,14 @@ def tile_bipartiteneuralmessagepassinglayer_pa_t_kernel(
                 transpose_x(k + 1)
             if live(k - 2) and vector_sums(k - 2):
                 sum_a(k - 2, 0, VECTOR_SUM_BLOCKS if k == NC - 1 else 2)
+            if live(k + 2) and splits(k + 2):
+                split_words(k + 2, nc.vector.tensor_copy, 0, splits(k + 2) - SPLIT_SCALAR)
             if live(k - 1):
                 quant_h(k - 1)
             if live(k - 2) and k < NC + 1:
                 back(k - 2)
             if live(k + 2) and splits(k + 2):
-                split_words(k + 2)
+                split_words(k + 2, nc.scalar.copy, splits(k + 2) - SPLIT_SCALAR, splits(k + 2))
             if k == 0:
                 prep_we2_regroup()
             if live(k):

@@ -30,10 +30,10 @@ FLOPS = 2 * NA * NB * K1 * ED + 2 * NA * NB * ED * ED
 TILES = (2, 2, 4, 4, 4, 4, 4, 4, 2, 2)
 VECTOR_SUM_BLOCKS = 3
 LAST = 2
-SPLIT = 3
+SPLIT = 4
 SPLIT_FROM = 3
 SPLIT_SHORT = 1
-SPLIT_SCALAR = 1
+SPLIT_SCALAR = 2
 ACC_LAG = 3
 
 
@@ -177,13 +177,19 @@ def tile_bipartiteneuralmessagepassinglayer_pa_t_kernel(
         hq = {}
         hsc = {}
         lt = {}
+        hs = {}
         lo = {}
 
         def live(c):
             return 0 <= c < NC
 
         def vector_sums(c):
+            if halved(c):
+                return BLOCKS
             return VECTOR_SUM_BLOCKS if c < NC - LAST else 0
+
+        def halved(c):
+            return 0 <= c and c + 2 < NC - LAST
 
         def splits(c):
             if c < SPLIT_FROM:
@@ -320,11 +326,28 @@ def tile_bipartiteneuralmessagepassinglayer_pa_t_kernel(
                         accum_out=st[:, m, i : i + 1],
                     )
 
-        def sum_a(c, m0, m1, step=1):
+        def sums_open(c):
+            hs[c] = work.tile([P, BLOCKS, 2 * TILES[c], NB // 2], F32, name="hs%d" % c, tag="hs", align_bytes=64)
+            nc.vector.memset(hs[c][:, 0, 0, :], 0.0)
+
+        def sums_half(c):
+            for m in range(BLOCKS):
+                x = lt[c][:, m, :].rearrange("p (i j) -> p i j", j=NB)
+                nc.gpsimd.tensor_tensor(
+                    out=hs[c][:, m, :, :], in0=x[:, :, 0 : NB // 2], in1=x[:, :, NB // 2 : NB], op=ADD
+                )
+
+        def sums_end(c):
             i0 = 2 * first_tile[c]
             nc.vector.tensor_reduce(
-                out=st[:, m0:m1:step, i0 : i0 + 2 * TILES[c]],
-                in_=lt[c][:, m0:m1:step, :].rearrange("p m (i j) -> p m i j", j=NB),
+                out=st[:, :, i0 : i0 + 2 * TILES[c]], in_=hs[c][:], axis=AX_X, op=ADD
+            )
+
+        def sum_a(c, ms):
+            i0 = 2 * first_tile[c]
+            nc.vector.tensor_reduce(
+                out=st[:, ms, i0 : i0 + 2 * TILES[c]],
+                in_=lt[c][:, ms, :].rearrange("p m (i j) -> p m i j", j=NB),
                 axis=AX_X,
                 op=ADD,
             )
@@ -373,6 +396,8 @@ def tile_bipartiteneuralmessagepassinglayer_pa_t_kernel(
         for k in range(NC + 2):
             if live(k - 1):
                 relu_regroup(k - 1)
+            if k == 1:
+                prep_we2_quant()
             if live(k - ACC_LAG):
                 accumulate(k - ACC_LAG)
             if k == NC + 1:
@@ -380,33 +405,35 @@ def tile_bipartiteneuralmessagepassinglayer_pa_t_kernel(
                     accumulate(c)
             if live(k + 1):
                 transpose_x(k + 1)
-            if live(k - 2) and vector_sums(k - 2):
-                sum_a(k - 2, 0, VECTOR_SUM_BLOCKS if k == NC - 1 else 2)
             if live(k + 2) and splits(k + 2):
-                split_words(k + 2, nc.vector.tensor_copy, 0, splits(k + 2) - SPLIT_SCALAR)
+                split_words(k + 2, nc.vector.tensor_copy, 0, max(0, splits(k + 2) - SPLIT_SCALAR))
+            if live(k - 2) and not halved(k - 2) and vector_sums(k - 2):
+                sum_a(k - 2, slice(0, VECTOR_SUM_BLOCKS))
             if live(k - 1):
                 quant_h(k - 1)
             if live(k - 2) and k < NC + 1:
                 back(k - 2)
             if live(k + 2) and splits(k + 2):
-                split_words(k + 2, nc.scalar.copy, splits(k + 2) - SPLIT_SCALAR, splits(k + 2))
+                split_words(k + 2, nc.scalar.copy, max(0, splits(k + 2) - SPLIT_SCALAR), splits(k + 2))
             if k == 0:
                 prep_we2_regroup()
+            if live(k - 2) and halved(k - 2):
+                sums_open(k - 2)
+                sums_half(k - 2)
             if live(k):
                 for m in range(BLOCKS):
                     stage1(k, m)
+            if halved(k - 3):
+                sums_end(k - 3)
             if live(k + 1):
                 quant_x(k + 1)
             if k == 0:
                 be2_columns()
-                prep_we2_quant()
             if live(k - 1):
                 for m in range(BLOCKS):
                     stage2(k - 1, m)
             if k == NC:
-                sum_a(NC - 1, 1, BLOCKS, 2)
-            if live(k - 2) and vector_sums(k - 2) and k < NC - 1:
-                sum_a(k - 2, 2, VECTOR_SUM_BLOCKS)
+                sum_a(NC - 1, slice(1, BLOCKS, 2))
 
         acc_sb = const.tile([P, ED], F32, name="acc_sb")
         so_a = const.tile([P, ED], F32, name="so_a")

from contextlib import ExitStack

import concourse.mybir as mybir
from concourse.masks import make_identity

F32 = mybir.dt.float32
BF16 = mybir.dt.bfloat16
U32 = mybir.dt.uint32
U8 = mybir.dt.uint8
FP8X4 = mybir.dt.float8_e4m3fn_x4
MAX = mybir.AluOpType.max
ADD = mybir.AluOpType.add
AX_X = mybir.AxisListType.X
RELU = mybir.ActivationFunctionType.Relu
IDENTITY = mybir.ActivationFunctionType.Identity

P = 128
NA = 64
NB = 64
K1 = 1024
ED = 512
BLOCKS = ED // P
PACK = 4
PASSES = K1 // (P * PACK)
ALL_TILES = NA * NB // P
BANK = 512
PAIR = 2 * P
FLOPS = 2 * NA * NB * K1 * ED + 2 * NA * NB * ED * ED

TILES = (2, 2, 4, 4, 4, 4, 4, 4, 2, 2)
VECTOR_SUM_BLOCKS = 3
LAST = 2
SPLIT = 4
SPLIT_FROM = 3
SPLIT_SHORT = 1
SPLIT_SCALAR = 2
ACC_LAG = 3


def tile_bipartiteneuralmessagepassinglayer_pa_t_kernel(
    tc, edge_embeds, a_proj, b_proj, We, be1, We2, be2, out_0, out_1, out_2
):
    nc = tc.nc
    x_rows = edge_embeds.rearrange("i j k -> (i j) k")
    o_rows = out_0.rearrange("i j f -> (i j) f")
    NC = len(TILES)
    first_tile = [sum(TILES[:c]) for c in range(NC)]
    assert sum(TILES) == ALL_TILES

    with ExitStack() as ctx:
        const = ctx.enter_context(tc.tile_pool(name="const", bufs=1))
        work = ctx.enter_context(tc.tile_pool(name="work", bufs=2))
        psum = ctx.enter_context(tc.psum_pool(name="psum", bufs=7))
        psacc = ctx.enter_context(tc.psum_pool(name="psacc", bufs=1))
        ctx.enter_context(tc.manual_schedule())

        def bank(label):
            return psum.tile([P, BANK], F32, tag="bank", name=label)

        ab_bf = const.tile([P, ED], BF16, name="ab_bf")
        be1_bf = const.tile([P, PACK], BF16, name="be1_bf")
        be2_bf = const.tile([P, P], BF16, name="be2_bf")
        nc.vector.memset(be2_bf[:], 0.0)
        warm = const.tile([P, 2], F32, name="warm")
        nc.vector.memset(warm[:], 0.0)
        nc.scalar.activation(out=warm[:, 1:2], in_=warm[:, 0:1], func=RELU)
        zeros = const.tile([P, BANK], BF16, name="zeros")
        nc.vector.memset(zeros[:], 0.0)
        ident = const.tile([P, P], F32, name="ident")
        make_identity(nc, ident[:])
        ident_bf = const.tile([P, P], BF16, name="ident_bf")
        nc.vector.tensor_copy(out=ident_bf[:], in_=ident[:])
        acc = psacc.tile([P, ED], F32, name="acc")
        idle = bank("idle")

        def warm_up(passes):
            for n in range(passes):
                nc.tensor.matmul(out=idle[:], lhsT=zeros[:, 0:P], rhs=zeros[:], start=True, stop=True)

        warm_up(8)

        xs = const.tile([P, ALL_TILES, K1], BF16, name="xs")
        wraw = const.tile([P, PASSES, PACK, ED], BF16, name="wraw")
        w2raw = const.tile([P, PACK, ED], BF16, name="w2raw")

        def load_x(t):
            rows = x_rows[t * P : (t + 2) * P, :]
            nc.sync.dma_start(out=xs[:, t : t + 2, :], in_=rows.rearrange("(t p) k -> p t k", p=P))

        def load_w(g):
            rows = We[g * P * PACK : (g + 1) * P * PACK, :]
            nc.sync.dma_start(out=wraw[:, g, :, :], in_=rows.rearrange("(p t) c -> p t c", t=PACK))

        load_w(0)
        load_x(0)
        load_w(1)
        nc.sync.dma_start(out=ab_bf[0:NA, :], in_=a_proj)
        nc.sync.dma_start(out=ab_bf[NA:P, :], in_=b_proj)
        nc.sync.dma_start(out=be1_bf[:], in_=be1.rearrange("(p t) -> p t", t=PACK))
        load_x(2)
        load_x(4)
        nc.sync.dma_start(out=be2_bf[0:BLOCKS, :], in_=be2.rearrange("(m f) -> m f", m=BLOCKS))
        nc.sync.dma_start(out=w2raw[:], in_=We2.rearrange("(p t) c -> p t c", t=PACK))
        for t in range(6, ALL_TILES, 2):
            load_x(t)

        abT = const.tile([P, PACK, P], F32, name="abT")
        be2T = const.tile([P, BLOCKS], F32, name="be2T")
        st = const.tile([P, BLOCKS, P], F32, name="st")
        sel = const.tile([P, P], F32, name="sel")
        nc.gpsimd.memset(st[:], 0.0)
        for half in range(2):
            nc.gpsimd.tensor_tensor(
                out=sel[:, half * NB : (half + 1) * NB], in0=ident[:, 0:NB], in1=ident[:, NB:P], op=ADD
            )

        def small_inputs_transpose():
            ps_ab = psum.tile([P, PACK, P], BF16, tag="bank", name="ps_ab")
            for t in range(PACK):
                nc.tensor.transpose(ps_ab[:, t, :], ab_bf[:, t:ED:PACK], ident_bf[:])
            return ps_ab

        def small_inputs_finish(ps_ab):
            nc.scalar.copy(out=abT[:, :, 0:NA], in_=ps_ab[:, :, 0:NA])
            for t in range(PACK):
                nc.scalar.activation(
                    out=abT[:, t, NA:P],
                    in_=ps_ab[:, t, NA:P],
                    func=IDENTITY,
                    bias=be1_bf[:, t : t + 1],
                    scale=1.0,
                )

        def be2_columns():
            ps_be2 = psum.tile([P, P], BF16, tag="bank", name="ps_be2")
            nc.tensor.transpose(ps_be2[:], be2_bf[:], ident_bf[:])
            nc.scalar.copy(out=be2T[:], in_=ps_be2[:, 0:BLOCKS])

        wg = const.tile([P, PASSES, ED, PACK], BF16, name="wg", align_bytes=64)
        wq = const.tile([P, PASSES * ED], U32, name="wq", align_bytes=64)
        wsc = const.tile([P, PASSES * ED], U8, name="wsc", align_bytes=64)
        w2g = const.tile([P, ED, PACK], BF16, name="w2g", align_bytes=64)
        w2q = const.tile([P, ED], U32, name="w2q", align_bytes=64)
        w2sc = const.tile([P, ED], U8, name="w2sc", align_bytes=64)

        def regroup(eng_copy, dst, src, t0, t1):
            eng_copy(
                out=dst[:, t0 * P : t1 * P, :].rearrange("p (t m) j -> p t m j", m=P),
                in_=src.rearrange("p j (m t) -> p t m j", t=PACK)[:, t0:t1, :, :],
            )

        def quant_we(g, t0, t1):
            cols = slice(g * ED + t0 * P, g * ED + t1 * P)
            nc.vector.quantize_mx(
                out=wq[:, cols].bitcast(FP8X4),
                scales=wsc[:, cols],
                in_=wg[:, g, t0 * P : t1 * P, :].rearrange("p c t -> p (c t)"),
            )

        def prep_we2_regroup():
            nc.scalar.copy(
                out=w2g[:].rearrange("p (c z) t -> p c t z", z=4),
                in_=w2raw[:].rearrange("p t (c z) -> p c t z", z=4),
            )

        def prep_we2_quant():
            nc.vector.quantize_mx(
                out=w2q[:].bitcast(FP8X4), scales=w2sc[:], in_=w2g[:].rearrange("p c t -> p (c t)")
            )

        xp = {}
        xg = {}
        xq = {}
        xsc = {}
        yy = {}
        hg = {}
        hq = {}
        hsc = {}
        lt = {}
        hs = {}
        lo = {}

        def live(c):
            return 0 <= c < NC

        def vector_sums(c):
            if halved(c):
                return BLOCKS
            return VECTOR_SUM_BLOCKS if c < NC - LAST else 0

        def halved(c):
            return 0 <= c and c + 2 < NC - LAST

        def splits(c):
            if c < SPLIT_FROM:
                return 0
            return SPLIT if TILES[c] == 4 else SPLIT_SHORT

        def split_words(c, copy, a, b):
            t0 = first_tile[c]
            if c not in xp:
                xp[c] = work.tile([P, splits(c), PASSES, 2, P], F32, name="xp%d" % c, tag="xp", align_bytes=64)
            if a < b:
                copy(
                    out=xp[c][:, a:b, :, :, :].rearrange("p t g u w -> p (t g) u w"),
                    in_=xs[:, t0 + a : t0 + b, :].bitcast(F32).rearrange("p t (g w u) -> p (t g) u w", g=PASSES, u=2),
                )

        def x_words(c, tl, g, u):
            if tl < splits(c):
                return xp[c][:, tl, g, u, :]
            words = xs[:, first_tile[c] + tl, :].bitcast(F32)
            return words[:, 2 * P * g + u : 2 * P * (g + 1) : 2]

        def transpose_x(c):
            n = TILES[c] * P
            xg[c] = work.tile([P, PASSES, n, 2], F32, name="xg%d" % c, tag="xg", align_bytes=64)
            for pair in range(TILES[c] // 2):
                for g in range(PASSES):
                    pb = bank("xt%d_%d_%d" % (c, g, pair))
                    for u in range(2):
                        for side in range(2):
                            nc.tensor.transpose(
                                pb[:, u * PAIR + side * P : u * PAIR + (side + 1) * P],
                                x_words(c, 2 * pair + side, g, u),
                                ident[:],
                            )
                    nc.scalar.copy(
                        out=xg[c][:, g, pair * PAIR : (pair + 1) * PAIR, :],
                        in_=pb[:].rearrange("p (u e) -> p e u", u=2),
                    )

        def quant_x(c):
            n = TILES[c] * P
            xq[c] = work.tile([P, PASSES * n], U32, name="xq%d" % c, tag="xq", align_bytes=64)
            xsc[c] = work.tile([P, PASSES * n], U8, name="xsc%d" % c, tag="xsc", align_bytes=64)
            nc.vector.quantize_mx(
                out=xq[c][:].bitcast(FP8X4),
                scales=xsc[c][:],
                in_=xg[c][:].rearrange("p g e u -> p (g e u)").bitcast(BF16),
            )

        def stage1(c, m):
            n = TILES[c] * P
            if m == 0:
                yy[c] = work.tile([P, BLOCKS, n], BF16, name="y%d" % c, tag="y")
            pb = bank("p1_%d_%d" % (c, m))
            for g in range(PASSES):
                cols = slice(g * ED + m * P, g * ED + (m + 1) * P)
                nc.tensor.matmul_mx(
                    out=pb[:, 0:n],
                    lhsT=wq[:, cols].bitcast(FP8X4),
                    lhsT_scale=wsc[:, cols],
                    rhs=xq[c][:, g * n : (g + 1) * n].bitcast(FP8X4),
                    rhs_scale=xsc[c][:, g * n : (g + 1) * n],
                    start=(g == 0),
                    stop=(g == PASSES - 1),
                )
            for il in range(2 * TILES[c]):
                i = 2 * first_tile[c] + il
                nc.vector.scalar_tensor_tensor(
                    out=yy[c][:, m, il * NB : (il + 1) * NB],
                    in0=pb[:, il * NB : (il + 1) * NB],
                    scalar=abT[:, m, i : i + 1],
                    in1=abT[:, m, NA:P],
                    op0=ADD,
                    op1=ADD,
                )

        def relu_regroup(c):
            n = TILES[c] * P
            hg[c] = work.tile([P, n, PACK], BF16, name="hg%d" % c, tag="hg", align_bytes=64)
            nc.vector.tensor_scalar_max(
                out=hg[c][:].rearrange("p (c z) t -> p c t z", z=4),
                in0=yy[c][:].rearrange("p t (c z) -> p c t z", z=4),
                scalar1=0.0,
            )

        def quant_h(c):
            n = TILES[c] * P
            hq[c] = work.tile([P, n], U32, name="hq%d" % c, tag="hq", align_bytes=64)
            hsc[c] = work.tile([P, n], U8, name="hsc%d" % c, tag="hsc", align_bytes=64)
            nc.vector.quantize_mx(
                out=hq[c][:].bitcast(FP8X4),
                scales=hsc[c][:],
                in_=hg[c][:].rearrange("p e t -> p (e t)"),
            )

        def stage2(c, m):
            n = TILES[c] * P
            if m == 0:
                lt[c] = work.tile([P, BLOCKS, n], F32, name="lt%d" % c, tag="lt", bufs=ACC_LAG)
            pb = bank("p2_%d_%d" % (c, m))
            cols = slice(m * P, (m + 1) * P)
            nc.tensor.matmul_mx(
                out=pb[:, 0:n],
                lhsT=w2q[:, cols].bitcast(FP8X4),
                lhsT_scale=w2sc[:, cols],
                rhs=hq[c][:].bitcast(FP8X4),
                rhs_scale=hsc[c][:],
                start=True,
                stop=True,
            )
            if c == NC - 1 and m % 2 == 1:
                nc.vector.tensor_scalar(
                    out=lt[c][:, m, :],
                    in0=pb[:, 0:n],
                    scalar1=be2T[:, m : m + 1],
                    scalar2=0.0,
                    op0=ADD,
                    op1=MAX,
                )
            elif m < vector_sums(c):
                nc.scalar.activation(
                    out=lt[c][:, m, :], in_=pb[:, 0:n], func=RELU, bias=be2T[:, m : m + 1], scale=1.0
                )
            else:
                for il in range(2 * TILES[c]):
                    i = 2 * first_tile[c] + il
                    nc.scalar.activation(
                        out=lt[c][:, m, il * NB : (il + 1) * NB],
                        in_=pb[:, il * NB : (il + 1) * NB],
                        func=RELU,
                        bias=be2T[:, m : m + 1],
                        scale=1.0,
                        accum_out=st[:, m, i : i + 1],
                    )

        def sums_open(c):
            hs[c] = work.tile([P, BLOCKS, 2 * TILES[c], NB // 2], F32, name="hs%d" % c, tag="hs", align_bytes=64)
            nc.vector.memset(hs[c][:, 0, 0, :], 0.0)

        def sums_half(c):
            for m in range(BLOCKS):
                x = lt[c][:, m, :].rearrange("p (i j) -> p i j", j=NB)
                nc.gpsimd.tensor_tensor(
                    out=hs[c][:, m, :, :], in0=x[:, :, 0 : NB // 2], in1=x[:, :, NB // 2 : NB], op=ADD
                )

        def sums_end(c):
            i0 = 2 * first_tile[c]
            nc.vector.tensor_reduce(
                out=st[:, :, i0 : i0 + 2 * TILES[c]], in_=hs[c][:], axis=AX_X, op=ADD
            )

        def sum_a(c, ms):
            i0 = 2 * first_tile[c]
            nc.vector.tensor_reduce(
                out=st[:, ms, i0 : i0 + 2 * TILES[c]],
                in_=lt[c][:, ms, :].rearrange("p m (i j) -> p m i j", j=NB),
                axis=AX_X,
                op=ADD,
            )

        def back(c):
            lo[c] = work.tile([P, TILES[c], ED], F32, name="lo%d" % c, tag="lo")
            r0 = first_tile[c] * P
            for tl in range(TILES[c]):
                pb = bank("lb%d_%d" % (c, tl))
                for m in range(BLOCKS):
                    nc.tensor.transpose(
                        pb[:, m * P : (m + 1) * P], lt[c][:, m, tl * P : (tl + 1) * P], ident[:]
                    )
                back_copy = nc.vector.tensor_copy if c >= NC - LAST and tl % 2 == 1 else nc.scalar.copy
                back_copy(out=lo[c][:, tl, :], in_=pb[:])
                if c == NC - 1:
                    nc.sync.dma_start(out=o_rows[r0 + tl * P : r0 + (tl + 1) * P, :], in_=lo[c][:, tl, :])
            if c < NC - 1:
                rows = o_rows[r0 : r0 + TILES[c] * P, :]
                nc.sync.dma_start(out=rows.rearrange("(t p) f -> p t f", p=P), in_=lo[c][:])

        def accumulate(c):
            for tl in range(TILES[c]):
                for m in range(BLOCKS):
                    nc.tensor.matmul(
                        out=acc[:, m * P : (m + 1) * P],
                        lhsT=lt[c][:, m, tl * P : (tl + 1) * P],
                        rhs=ident[:],
                        is_transpose=True,
                        start=(c == 0 and tl == 0 and m == 0),
                        stop=(c == NC - 1 and tl == TILES[c] - 1 and m == BLOCKS - 1),
                    )

        half = PACK // 2
        transpose_x(0)
        ps_ab = small_inputs_transpose()
        small_inputs_finish(ps_ab)
        warm_up(2)
        regroup(nc.vector.tensor_copy, wg[:, 0, :, :], wraw[:, 0, :, :], 0, PACK)
        quant_we(0, 0, PACK)
        regroup(nc.vector.tensor_copy, wg[:, 1, :, :], wraw[:, 1, :, :], 0, half)
        regroup(nc.vector.tensor_copy, wg[:, 1, :, :], wraw[:, 1, :, :], half, PACK)
        quant_x(0)
        quant_we(1, 0, half)
        quant_we(1, half, PACK)
        for k in range(NC + 2):
            if live(k - 1):
                relu_regroup(k - 1)
            if k == 1:
                prep_we2_quant()
            if live(k - ACC_LAG):
                accumulate(k - ACC_LAG)
            if k == NC + 1:
                for c in range(k - ACC_LAG + 1, NC):
                    accumulate(c)
            if live(k + 1):
                transpose_x(k + 1)
            if live(k + 2) and splits(k + 2):
                split_words(k + 2, nc.vector.tensor_copy, 0, max(0, splits(k + 2) - SPLIT_SCALAR))
            if live(k - 2) and not halved(k - 2) and vector_sums(k - 2):
                sum_a(k - 2, slice(0, VECTOR_SUM_BLOCKS))
            if live(k - 1):
                quant_h(k - 1)
            if live(k - 2) and k < NC + 1:
                back(k - 2)
            if live(k + 2) and splits(k + 2):
                split_words(k + 2, nc.scalar.copy, max(0, splits(k + 2) - SPLIT_SCALAR), splits(k + 2))
            if k == 0:
                prep_we2_regroup()
            if live(k - 2) and halved(k - 2):
                sums_open(k - 2)
                sums_half(k - 2)
            if live(k):
                for m in range(BLOCKS):
                    stage1(k, m)
            if halved(k - 3):
                sums_end(k - 3)
            if live(k + 1):
                quant_x(k + 1)
            if k == 0:
                be2_columns()
            if live(k - 1):
                for m in range(BLOCKS):
                    stage2(k - 1, m)
            if k == NC:
                sum_a(NC - 1, slice(1, BLOCKS, 2))

        acc_sb = const.tile([P, ED], F32, name="acc_sb")
        so_a = const.tile([P, ED], F32, name="so_a")
        so_b = const.tile([P, ED], F32, name="so_b")
        lo_half = slice(0, ED // 2)
        hi_half = slice(ED // 2, ED)
        nc.vector.tensor_copy(out=acc_sb[:, lo_half], in_=acc[:, lo_half])
        nc.vector.tensor_copy(out=acc_sb[:, hi_half], in_=acc[:, hi_half])
        back(NC - 1)
        pa = bank("ps_suma")
        for m in range(BLOCKS):
            nc.tensor.transpose(pa[:, m * P : (m + 1) * P], st[:, m, :], ident[:])
        for cols in (lo_half, hi_half):
            pb = bank("ps_sumb")
            nc.tensor.matmul(out=pb[:, cols], lhsT=sel[:], rhs=acc_sb[:, cols], start=True, stop=True)
            nc.vector.tensor_copy(out=so_b[:, cols], in_=pb[:, cols])
        nc.sync.dma_start(out=out_2, in_=so_b[0:NB, :])
        nc.scalar.copy(out=so_a[:], in_=pa[:])
        nc.scalar.dma_start(out=out_1, in_=so_a[0:NA, :])
